import numpy as np
import ml_dtypes


def mxq(x, axis, fmt="e4m3"):
    dtype, down = {"e4m3": (ml_dtypes.float8_e4m3fn, 7), "e5m2": (ml_dtypes.float8_e5m2, 14)}[fmt]
    v = np.moveaxis(np.asarray(x, np.float32).astype(ml_dtypes.bfloat16).astype(np.float64), axis, -1)
    blocks = v.reshape(v.shape[:-1] + (-1, 32))
    amax = np.abs(blocks).max(-1, keepdims=True)
    byte = np.maximum(np.where(amax > 0, np.frexp(amax)[1] - 1 + 127, 0) - down, 1)
    scale = np.exp2(byte - 127.0)
    codes = (blocks / scale).astype(np.float32).astype(dtype).astype(np.float64)
    return np.moveaxis((codes * scale).reshape(v.shape), -1, axis)


WIDE = False


def mx_kscale(k):
    if not WIDE:
        return np.ones(k)
    levels = np.array([10, -10, 5, -5, 0])
    a = np.random.permutation(np.resize(levels, k // 512 * 4)).reshape(k // 512, 4)
    idx = np.arange(k)
    return np.exp2(a[idx // 512, idx % 128 // 32])


BF16 = ml_dtypes.bfloat16


def bf(x):
    return np.asarray(x, np.float32).astype(BF16)


def f64(x):
    return np.asarray(x).astype(np.float64)


E2M1 = np.array([0.0, 0.5, 1.0, 1.5, 2.0, 3.0, 4.0, 6.0, -0.0, -0.5, -1.0, -1.5, -2.0, -3.0, -4.0, -6.0])


def pack_weight(w, fmt):
    k, n = w.shape
    w = f64(bf(w)).reshape(k // 32, 32, n)
    amax = np.abs(w).max(1)
    if fmt == "e4m3":
        byte = np.frexp(amax)[1] - 1 + 127 - 7
    else:
        mant, ex = np.frexp(amax / 6.0)
        byte = np.where(mant > 0.5, ex, ex - 1) + 127
    byte = np.clip(np.where(amax > 0, byte, 1), 1, 254)
    scaled = (w * np.exp2(127.0 - byte)[:, None, :]).reshape(k, n).astype(np.float32)
    by_word = np.ascontiguousarray(scaled.reshape(k // 512, 128, 4, n).transpose(0, 1, 3, 2))
    if fmt == "e4m3":
        words = by_word.astype(ml_dtypes.float8_e4m3fn).view(np.uint8)
    else:
        c = by_word.astype(ml_dtypes.float4_e2m1fn).view(np.uint8) & 0xF
        words = c[..., 0::2] | (c[..., 1::2] << 4)
    return np.ascontiguousarray(words), np.ascontiguousarray(byte.astype(np.uint8).reshape(k // 512, 16, n))


def unpack_weight(words, scales, fmt):
    g, p, n, _ = words.shape
    if fmt == "e4m3":
        vals = np.ascontiguousarray(words).view(ml_dtypes.float8_e4m3fn).astype(np.float64)
    else:
        nib = np.empty((g, p, n, 4), np.uint8)
        nib[..., 0::2] = words & 0xF
        nib[..., 1::2] = words >> 4
        vals = E2M1[nib]
    vals = vals * np.repeat(np.exp2(scales.astype(np.float64) - 127.0), 8, axis=1)[..., None]
    return vals.transpose(0, 1, 3, 2).reshape(g * 512, n)


T, D, E, BLK = 8192, 1024, 128, 512
EPS = 1e-05
FMT = "e4m3"


def setup_inputs():
    s = mx_kscale(D)
    rs = 10.0 ** np.random.uniform(-2.5, 0.5, (T, 1))
    h = bf((np.random.standard_normal((T, D)) + 0.3) * rs)
    ln_w = bf(np.random.standard_normal(D) * s)
    ln_b = bf(np.random.standard_normal(D) * 0.3 * s)
    w_q_words, w_q_scales = pack_weight(np.ascontiguousarray((np.random.standard_normal((E, D)) * 1.6 / np.sqrt(D) / s).T), FMT)
    w_k_words, w_k_scales = pack_weight(np.ascontiguousarray((np.random.standard_normal((E, D)) * 1.6 / np.sqrt(D) / s).T), FMT)
    w_v_words, w_v_scales = pack_weight(np.ascontiguousarray((np.random.standard_normal((E, D)) * 1.0 / np.sqrt(D) / s).T), FMT)
    return {"h": h,
            "ln_w": ln_w,
            "ln_b": ln_b,
            "w_q_words": w_q_words, "w_q_scales": w_q_scales,
            "w_k_words": w_k_words, "w_k_scales": w_k_scales,
            "w_v_words": w_v_words, "w_v_scales": w_v_scales}


def reference(h, ln_w, ln_b, w_q_words, w_q_scales, w_k_words, w_k_scales, w_v_words, w_v_scales):
    h = f64(h)
    mu = h.mean(-1, keepdims=True)
    var = np.square(h - mu).mean(-1, keepdims=True)
    h_norm = (h - mu) / np.sqrt(var + EPS) * f64(ln_w) + f64(ln_b)
    hq = mxq(h_norm, 1, "e4m3")
    q = hq @ unpack_weight(w_q_words, w_q_scales, FMT)
    k = hq @ unpack_weight(w_k_words, w_k_scales, FMT)
    v = hq @ unpack_weight(w_v_words, w_v_scales, FMT)
    return q, k, v

@@ -1,0 +1,219 @@
+from contextlib import ExitStack
+
+import concourse.mybir as mybir
+from concourse.masks import make_identity
+
+F32 = mybir.dt.float32
+BF16 = mybir.dt.bfloat16
+I32 = mybir.dt.int32
+U32 = mybir.dt.uint32
+U8 = mybir.dt.uint8
+FP8X4 = mybir.dt.float8_e4m3fn_x4
+ALU = mybir.AluOpType
+ACT = mybir.ActivationFunctionType
+
+T = 8192
+D = 1024
+E = 128
+EPS = 1e-5
+FLOPS = 2 * T * D * 3 * E
+
+P = 128
+PACK = 4
+K_PASS = P * PACK
+PASSES = D // K_PASS
+ROWS_PER_PARTITION = T // P
+TILES = 4
+GROUP_ROWS = TILES * P
+GROUPS = ROWS_PER_PARTITION // TILES
+BN_CHUNK = 512
+BN_CHUNKS = D // BN_CHUNK
+
+
+def tile_toyattnsublayer_pa_t_kernel(
+    tc, h, ln_w, ln_b, w_q_words, w_q_scales, w_k_words, w_k_scales, w_v_words, w_v_scales, out_0, out_1, out_2
+):
+    nc = tc.nc
+    weights = [(w_q_words, w_q_scales), (w_k_words, w_k_scales), (w_v_words, w_v_scales)]
+    outs = [out_0, out_1, out_2]
+    n_out = len(outs)
+
+    h_rows = h.rearrange("(p j) d -> p j d", j=ROWS_PER_PARTITION)
+    out_rows = [o.rearrange("(p j) e -> p j e", j=ROWS_PER_PARTITION) for o in outs]
+
+    with ExitStack() as ctx:
+        const = ctx.enter_context(tc.tile_pool(name="const", bufs=1))
+        h_pool = ctx.enter_context(tc.tile_pool(name="h_pool", bufs=5))
+        stat_pool = ctx.enter_context(tc.tile_pool(name="stat_pool", bufs=4))
+        xhat_pool = ctx.enter_context(tc.tile_pool(name="xhat_pool", bufs=2))
+        plane_pool = ctx.enter_context(tc.tile_pool(name="plane_pool", bufs=2 * PASSES))
+        grouped_pool = ctx.enter_context(tc.tile_pool(name="grouped_pool", bufs=PASSES))
+        mx_pool = ctx.enter_context(tc.tile_pool(name="mx_pool", bufs=2))
+        res_pool = ctx.enter_context(tc.tile_pool(name="res_pool", bufs=2))
+        psum_t = ctx.enter_context(tc.psum_pool(name="psum_t", bufs=5))
+        psum_o = ctx.enter_context(tc.psum_pool(name="psum_o", bufs=1))
+
+        h_tiles = {}
+        mean_var = {}
+        std = {}
+        neg_mean = {}
+        rstd = {}
+        xhat = {}
+        planes = {}
+        h_codes = {}
+        h_scales = {}
+
+        def load(a):
+            h_sb = h_pool.tile([P, TILES, D], BF16)
+            nc.sync.dma_start(out=h_sb[:], in_=h_rows[:, a * TILES : (a + 1) * TILES, :])
+            h_tiles[a] = h_sb
+
+        load(0)
+
+        ident = const.tile([P, P], F32)
+        make_identity(nc, ident[:])
+
+        w_bf = const.tile([P, PASSES, PACK], BF16)
+        b_bf = const.tile([P, PASSES, PACK], BF16)
+        nc.sync.dma_start(out=w_bf[:], in_=ln_w.rearrange("(g p t) -> p g t", g=PASSES, t=PACK))
+        nc.sync.dma_start(out=b_bf[:], in_=ln_b.rearrange("(g p t) -> p g t", g=PASSES, t=PACK))
+        gain = const.tile([P, PASSES, PACK], F32)
+        shift = const.tile([P, PASSES, PACK], F32)
+        nc.vector.tensor_copy(out=gain[:], in_=w_bf[:])
+        nc.vector.tensor_copy(out=shift[:], in_=b_bf[:])
+
+        w_codes = const.tile([P, PASSES, n_out, E], U32, align_bytes=64)
+        w_planes = const.tile([P, PASSES, n_out, E], U8, align_bytes=64)
+        nc.vector.memset(w_planes[:].rearrange("p g o n -> p (g o n)").bitcast(I32), 0)
+        for o in range(n_out):
+            words, scales = weights[o]
+            nc.sync.dma_start(
+                out=w_codes[:, :, o, :].bitcast(I32),
+                in_=words.rearrange("g p n t -> p g (n t)").bitcast(I32),
+            )
+            for quadrant in range(4):
+                nc.sync.dma_start(
+                    out=w_planes[32 * quadrant : 32 * quadrant + 4, :, o, :].bitcast(I32),
+                    in_=scales[:, 4 * quadrant : 4 * quadrant + 4, :].rearrange("g q n -> q g n").bitcast(I32),
+                )
+
+        load(1)
+
+        def statistics(a):
+            h_sb = h_tiles[a]
+            chunk_stats = stat_pool.tile([P, TILES, BN_CHUNKS, 6], F32)
+            mv = stat_pool.tile([P, TILES, 2], F32)
+            for j in range(TILES):
+                for c in range(BN_CHUNKS):
+                    nc.vector.bn_stats(out=chunk_stats[:, j, c, :], in_=h_sb[:, j, c * BN_CHUNK : (c + 1) * BN_CHUNK])
+            for j in range(TILES):
+                nc.vector.bn_aggr(out=mv[:, j, :], in_=chunk_stats[:, j, :, :].rearrange("p c s -> p (c s)"))
+            minus_mu = stat_pool.tile([P, TILES], F32)
+            nc.vector.tensor_scalar(out=minus_mu[:], in0=mv[:, :, 0], scalar1=-1.0, scalar2=None, op0=ALU.mult)
+            mean_var[a] = mv
+            neg_mean[a] = minus_mu
+
+        def root(a):
+            sd = stat_pool.tile([P, TILES], F32)
+            nc.scalar.activation(out=sd[:], in_=mean_var[a][:, :, 1], func=ACT.Sqrt, bias=EPS, scale=1.0)
+            std[a] = sd
+
+        def inverse(a):
+            inv = stat_pool.tile([P, TILES], F32)
+            nc.vector.reciprocal(out=inv[:], in_=std[a][:])
+            rstd[a] = inv
+
+        def normalise(a):
+            h_sb = h_tiles[a]
+            xh = xhat_pool.tile([P, TILES, D], F32)
+            for j in range(TILES):
+                nc.gpsimd.tensor_scalar(
+                    out=xh[:, j, :],
+                    in0=h_sb[:, j, :],
+                    scalar1=neg_mean[a][:, j : j + 1],
+                    scalar2=rstd[a][:, j : j + 1],
+                    op0=ALU.add,
+                    op1=ALU.mult,
+                )
+            xhat[a] = xh
+
+        def transpose_and_scale(a):
+            xh = xhat[a]
+            for g in range(PASSES):
+                plane = plane_pool.tile([P, PACK, GROUP_ROWS], BF16)
+                for t in range(PACK):
+                    xt = psum_t.tile([P, GROUP_ROWS], F32)
+                    for j in range(TILES):
+                        nc.tensor.transpose(
+                            xt[:, j * P : (j + 1) * P],
+                            xh[:, j, g * K_PASS + t : (g + 1) * K_PASS : PACK],
+                            ident[:],
+                        )
+                    nc.scalar.activation(
+                        out=plane[:, t, :],
+                        in_=xt[:],
+                        func=ACT.Identity,
+                        scale=gain[:, g, t : t + 1],
+                        bias=shift[:, g, t : t + 1],
+                    )
+                planes[(a, g)] = plane
+
+        def quantise(a):
+            codes = mx_pool.tile([P, PASSES, GROUP_ROWS], U32, align_bytes=64)
+            scales = mx_pool.tile([P, PASSES, GROUP_ROWS], U8, align_bytes=64)
+            grouped = []
+            for g in range(PASSES):
+                side_by_side = grouped_pool.tile([P, GROUP_ROWS, PACK], BF16, align_bytes=64)
+                nc.vector.tensor_copy(
+                    out=side_by_side[:].rearrange("p (c i) t -> p c t i", i=4),
+                    in_=planes[(a, g)][:].rearrange("p t (c i) -> p c t i", i=4),
+                )
+                grouped.append(side_by_side)
+            for g in range(PASSES):
+                nc.vector.quantize_mx(
+                    out=codes[:, g, :].bitcast(FP8X4),
+                    scales=scales[:, g, :],
+                    in_=grouped[g][:].rearrange("p r t -> p (r t)"),
+                )
+            h_codes[a] = codes
+            h_scales[a] = scales
+
+        def project_and_store(a):
+            for o in range(n_out):
+                acc = psum_o.tile([P, TILES * E], F32, name="acc%d" % o)
+                for j in range(TILES):
+                    for g in range(PASSES):
+                        nc.tensor.matmul_mx(
+                            out=acc[:, j * E : (j + 1) * E],
+                            lhsT=h_codes[a][:, g, j * P : (j + 1) * P].bitcast(FP8X4),
+                            lhsT_scale=h_scales[a][:, g, j * P : (j + 1) * P],
+                            rhs=w_codes[:, g, o, :].bitcast(FP8X4),
+                            rhs_scale=w_planes[:, g, o, :],
+                            start=(g == 0),
+                            stop=(g == PASSES - 1),
+                        )
+                res = res_pool.tile([P, TILES, E], F32, name="res%d" % o)
+                nc.scalar.copy(out=res[:].rearrange("p j e -> p (j e)"), in_=acc[:])
+                nc.sync.dma_start(out=out_rows[o][:, a * TILES : (a + 1) * TILES, :], in_=res[:])
+
+        def in_range(a):
+            return 0 <= a < GROUPS
+
+        with tc.manual_schedule():
+            for step in range(GROUPS + 5):
+                if in_range(step + 2) and step + 2 >= 2:
+                    load(step + 2)
+                if in_range(step - 1):
+                    root(step - 1)
+                if in_range(step - 4):
+                    quantise(step - 4)
+                if in_range(step - 1):
+                    inverse(step - 1)
+                if in_range(step):
+                    statistics(step)
+                if in_range(step - 2):
+                    normalise(step - 2)
+                if in_range(step - 3):
+                    transpose_and_scale(step - 3)
+                if in_range(step - 5):
+                    project_and_store(step - 5)

@@ -28,6 +28,8 @@ GROUP_ROWS = TILES * P
 GROUPS = ROWS_PER_PARTITION // TILES
 BN_CHUNK = 512
 BN_CHUNKS = D // BN_CHUNK
+VECTOR_ROWS = 3 * P
+QUANTISE_LAG = 6
 
 
 def tile_toyattnsublayer_pa_t_kernel(
@@ -46,7 +48,7 @@ def tile_toyattnsublayer_pa_t_kernel(
         h_pool = ctx.enter_context(tc.tile_pool(name="h_pool", bufs=5))
         stat_pool = ctx.enter_context(tc.tile_pool(name="stat_pool", bufs=4))
         xhat_pool = ctx.enter_context(tc.tile_pool(name="xhat_pool", bufs=2))
-        plane_pool = ctx.enter_context(tc.tile_pool(name="plane_pool", bufs=2 * PASSES))
+        plane_pool = ctx.enter_context(tc.tile_pool(name="plane_pool", bufs=(QUANTISE_LAG - 2) * PASSES))
         grouped_pool = ctx.enter_context(tc.tile_pool(name="grouped_pool", bufs=PASSES))
         mx_pool = ctx.enter_context(tc.tile_pool(name="mx_pool", bufs=2))
         res_pool = ctx.enter_context(tc.tile_pool(name="res_pool", bufs=2))
@@ -65,7 +67,8 @@ def tile_toyattnsublayer_pa_t_kernel(
 
         def load(a):
             h_sb = h_pool.tile([P, TILES, D], BF16)
-            nc.sync.dma_start(out=h_sb[:], in_=h_rows[:, a * TILES : (a + 1) * TILES, :])
+            for j in range(TILES):
+                nc.sync.dma_start(out=h_sb[:, j, :], in_=h_rows[:, a * TILES + j, :])
             h_tiles[a] = h_sb
 
         load(0)
@@ -108,15 +111,15 @@ def tile_toyattnsublayer_pa_t_kernel(
                     nc.vector.bn_stats(out=chunk_stats[:, j, c, :], in_=h_sb[:, j, c * BN_CHUNK : (c + 1) * BN_CHUNK])
             for j in range(TILES):
                 nc.vector.bn_aggr(out=mv[:, j, :], in_=chunk_stats[:, j, :, :].rearrange("p c s -> p (c s)"))
-            minus_mu = stat_pool.tile([P, TILES], F32)
-            nc.vector.tensor_scalar(out=minus_mu[:], in0=mv[:, :, 0], scalar1=-1.0, scalar2=None, op0=ALU.mult)
             mean_var[a] = mv
-            neg_mean[a] = minus_mu
 
         def root(a):
             sd = stat_pool.tile([P, TILES], F32)
             nc.scalar.activation(out=sd[:], in_=mean_var[a][:, :, 1], func=ACT.Sqrt, bias=EPS, scale=1.0)
+            minus_mu = stat_pool.tile([P, TILES], F32)
+            nc.scalar.mul(out=minus_mu[:], in_=mean_var[a][:, :, 0], mul=-1.0)
             std[a] = sd
+            neg_mean[a] = minus_mu
 
         def inverse(a):
             inv = stat_pool.tile([P, TILES], F32)
@@ -165,8 +168,12 @@ def tile_toyattnsublayer_pa_t_kernel(
             for g in range(PASSES):
                 side_by_side = grouped_pool.tile([P, GROUP_ROWS, PACK], BF16, align_bytes=64)
                 nc.vector.tensor_copy(
-                    out=side_by_side[:].rearrange("p (c i) t -> p c t i", i=4),
-                    in_=planes[(a, g)][:].rearrange("p t (c i) -> p c t i", i=4),
+                    out=side_by_side[:, :VECTOR_ROWS, :].rearrange("p (c i) t -> p c t i", i=4),
+                    in_=planes[(a, g)][:, :, :VECTOR_ROWS].rearrange("p t (c i) -> p c t i", i=4),
+                )
+                nc.scalar.copy(
+                    out=side_by_side[:, VECTOR_ROWS:, :].rearrange("p (c i) t -> p c t i", i=4),
+                    in_=planes[(a, g)][:, :, VECTOR_ROWS:].rearrange("p t (c i) -> p c t i", i=4),
                 )
                 grouped.append(side_by_side)
             for g in range(PASSES):
@@ -200,20 +207,20 @@ def tile_toyattnsublayer_pa_t_kernel(
             return 0 <= a < GROUPS
 
         with tc.manual_schedule():
-            for step in range(GROUPS + 5):
+            for step in range(GROUPS + QUANTISE_LAG + 1):
                 if in_range(step + 2) and step + 2 >= 2:
                     load(step + 2)
                 if in_range(step - 1):
                     root(step - 1)
-                if in_range(step - 4):
-                    quantise(step - 4)
-                if in_range(step - 1):
-                    inverse(step - 1)
+                if in_range(step - QUANTISE_LAG):
+                    quantise(step - QUANTISE_LAG)
                 if in_range(step):
                     statistics(step)
+                if in_range(step - 1):
+                    inverse(step - 1)
                 if in_range(step - 2):
                     normalise(step - 2)
+                if in_range(step - QUANTISE_LAG - 1):
+                    project_and_store(step - QUANTISE_LAG - 1)
                 if in_range(step - 3):
                     transpose_and_scale(step - 3)
-                if in_range(step - 5):
-                    project_and_store(step - 5)

@@ -28,8 +28,9 @@ GROUP_ROWS = TILES * P
 GROUPS = ROWS_PER_PARTITION // TILES
 BN_CHUNK = 512
 BN_CHUNKS = D // BN_CHUNK
-VECTOR_ROWS = 3 * P
-QUANTISE_LAG = 6
+HALF_TILES = TILES // 2
+GPSIMD_TILES = 3
+QUANTISE_LAG = 4
 
 
 def tile_toyattnsublayer_pa_t_kernel(
@@ -47,7 +48,7 @@ def tile_toyattnsublayer_pa_t_kernel(
         const = ctx.enter_context(tc.tile_pool(name="const", bufs=1))
         h_pool = ctx.enter_context(tc.tile_pool(name="h_pool", bufs=5))
         stat_pool = ctx.enter_context(tc.tile_pool(name="stat_pool", bufs=4))
-        xhat_pool = ctx.enter_context(tc.tile_pool(name="xhat_pool", bufs=2))
+        xhat_pool = ctx.enter_context(tc.tile_pool(name="xhat_pool", bufs=3))
         plane_pool = ctx.enter_context(tc.tile_pool(name="plane_pool", bufs=(QUANTISE_LAG - 2) * PASSES))
         grouped_pool = ctx.enter_context(tc.tile_pool(name="grouped_pool", bufs=PASSES))
         mx_pool = ctx.enter_context(tc.tile_pool(name="mx_pool", bufs=2))
@@ -60,6 +61,8 @@ def tile_toyattnsublayer_pa_t_kernel(
         std = {}
         neg_mean = {}
         rstd = {}
+        neg_mean_rstd = {}
+        accumulators = {}
         xhat = {}
         planes = {}
         h_codes = {}
@@ -124,15 +127,18 @@ def tile_toyattnsublayer_pa_t_kernel(
         def inverse(a):
             inv = stat_pool.tile([P, TILES], F32)
             nc.vector.reciprocal(out=inv[:], in_=std[a][:])
+            minus_mu_rstd = stat_pool.tile([P, TILES], F32)
+            nc.vector.tensor_tensor(out=minus_mu_rstd[:], in0=neg_mean[a][:], in1=inv[:], op=ALU.mult)
             rstd[a] = inv
+            neg_mean_rstd[a] = minus_mu_rstd
 
-        def normalise(a):
-            h_sb = h_tiles[a]
+        def normalise_three_tiles(a):
+            engine = nc.vector if a == GROUPS - 1 else nc.gpsimd
             xh = xhat_pool.tile([P, TILES, D], F32)
-            for j in range(TILES):
-                nc.gpsimd.tensor_scalar(
+            for j in range(GPSIMD_TILES):
+                engine.tensor_scalar(
                     out=xh[:, j, :],
-                    in0=h_sb[:, j, :],
+                    in0=h_tiles[a][:, j, :],
                     scalar1=neg_mean[a][:, j : j + 1],
                     scalar2=rstd[a][:, j : j + 1],
                     op0=ALU.add,
@@ -140,26 +146,34 @@ def tile_toyattnsublayer_pa_t_kernel(
                 )
             xhat[a] = xh
 
-        def transpose_and_scale(a):
-            xh = xhat[a]
-            for g in range(PASSES):
-                plane = plane_pool.tile([P, PACK, GROUP_ROWS], BF16)
-                for t in range(PACK):
-                    xt = psum_t.tile([P, GROUP_ROWS], F32)
-                    for j in range(TILES):
-                        nc.tensor.transpose(
-                            xt[:, j * P : (j + 1) * P],
-                            xh[:, j, g * K_PASS + t : (g + 1) * K_PASS : PACK],
-                            ident[:],
-                        )
-                    nc.scalar.activation(
-                        out=plane[:, t, :],
-                        in_=xt[:],
-                        func=ACT.Identity,
-                        scale=gain[:, g, t : t + 1],
-                        bias=shift[:, g, t : t + 1],
+        def normalise_fourth_tile(a):
+            for j in range(GPSIMD_TILES, TILES):
+                nc.scalar.activation(
+                    out=xhat[a][:, j, :],
+                    in_=h_tiles[a][:, j, :],
+                    func=ACT.Identity,
+                    scale=rstd[a][:, j : j + 1],
+                    bias=neg_mean_rstd[a][:, j : j + 1],
+                )
+
+        def transpose_and_scale(a, g):
+            plane = plane_pool.tile([P, PACK, GROUP_ROWS], BF16)
+            for t in range(PACK):
+                xt = psum_t.tile([P, GROUP_ROWS], F32)
+                for j in range(TILES):
+                    nc.tensor.transpose(
+                        xt[:, j * P : (j + 1) * P],
+                        xhat[a][:, j, g * K_PASS + t : (g + 1) * K_PASS : PACK],
+                        ident[:],
                     )
-                planes[(a, g)] = plane
+                nc.scalar.activation(
+                    out=plane[:, t, :],
+                    in_=xt[:],
+                    func=ACT.Identity,
+                    scale=gain[:, g, t : t + 1],
+                    bias=shift[:, g, t : t + 1],
+                )
+            planes[(a, g)] = plane
 
         def quantise(a):
             codes = mx_pool.tile([P, PASSES, GROUP_ROWS], U32, align_bytes=64)
@@ -168,12 +182,8 @@ def tile_toyattnsublayer_pa_t_kernel(
             for g in range(PASSES):
                 side_by_side = grouped_pool.tile([P, GROUP_ROWS, PACK], BF16, align_bytes=64)
                 nc.vector.tensor_copy(
-                    out=side_by_side[:, :VECTOR_ROWS, :].rearrange("p (c i) t -> p c t i", i=4),
-                    in_=planes[(a, g)][:, :, :VECTOR_ROWS].rearrange("p t (c i) -> p c t i", i=4),
-                )
-                nc.scalar.copy(
-                    out=side_by_side[:, VECTOR_ROWS:, :].rearrange("p (c i) t -> p c t i", i=4),
-                    in_=planes[(a, g)][:, :, VECTOR_ROWS:].rearrange("p t (c i) -> p c t i", i=4),
+                    out=side_by_side[:].rearrange("p (c i) t -> p c t i", i=4),
+                    in_=planes[(a, g)][:].rearrange("p t (c i) -> p c t i", i=4),
                 )
                 grouped.append(side_by_side)
             for g in range(PASSES):
@@ -185,13 +195,14 @@ def tile_toyattnsublayer_pa_t_kernel(
             h_codes[a] = codes
             h_scales[a] = scales
 
-        def project_and_store(a):
+        def project(a, half):
             for o in range(n_out):
-                acc = psum_o.tile([P, TILES * E], F32, name="acc%d" % o)
-                for j in range(TILES):
+                if half == 0:
+                    accumulators[(a, o)] = psum_o.tile([P, TILES * E], F32, name="acc%d" % o)
+                for j in range(half * HALF_TILES, (half + 1) * HALF_TILES):
                     for g in range(PASSES):
                         nc.tensor.matmul_mx(
-                            out=acc[:, j * E : (j + 1) * E],
+                            out=accumulators[(a, o)][:, j * E : (j + 1) * E],
                             lhsT=h_codes[a][:, g, j * P : (j + 1) * P].bitcast(FP8X4),
                             lhsT_scale=h_scales[a][:, g, j * P : (j + 1) * P],
                             rhs=w_codes[:, g, o, :].bitcast(FP8X4),
@@ -199,8 +210,11 @@ def tile_toyattnsublayer_pa_t_kernel(
                             start=(g == 0),
                             stop=(g == PASSES - 1),
                         )
+
+        def store(a):
+            for o in range(n_out):
                 res = res_pool.tile([P, TILES, E], F32, name="res%d" % o)
-                nc.scalar.copy(out=res[:].rearrange("p j e -> p (j e)"), in_=acc[:])
+                nc.scalar.copy(out=res[:].rearrange("p j e -> p (j e)"), in_=accumulators[(a, o)][:])
                 nc.sync.dma_start(out=out_rows[o][:, a * TILES : (a + 1) * TILES, :], in_=res[:])
 
         def in_range(a):
@@ -214,13 +228,17 @@ def tile_toyattnsublayer_pa_t_kernel(
                     root(step - 1)
                 if in_range(step - QUANTISE_LAG):
                     quantise(step - QUANTISE_LAG)
-                if in_range(step):
-                    statistics(step)
                 if in_range(step - 1):
                     inverse(step - 1)
-                if in_range(step - 2):
-                    normalise(step - 2)
+                    normalise_three_tiles(step - 1)
+                if in_range(step):
+                    statistics(step)
+                for half in range(PASSES):
+                    if in_range(step - 3):
+                        transpose_and_scale(step - 3, half)
+                    if in_range(step - QUANTISE_LAG - 1):
+                        project(step - QUANTISE_LAG - 1, half)
                 if in_range(step - QUANTISE_LAG - 1):
-                    project_and_store(step - QUANTISE_LAG - 1)
-                if in_range(step - 3):
-                    transpose_and_scale(step - 3)
+                    store(step - QUANTISE_LAG - 1)
+                if in_range(step - 1):
+                    normalise_fourth_tile(step - 1)

@@ -137,8 +137,8 @@ def tile_toyattnsublayer_pa_t_kernel(
             xh = xhat_pool.tile([P, TILES, D], F32)
             for j in range(GPSIMD_TILES):
                 engine.tensor_scalar(
-                    out=xh[:, j, :],
-                    in0=h_tiles[a][:, j, :],
+                    out=xh[:, j, :].rearrange("r (g t p) -> r g t p", g=PASSES, t=PACK),
+                    in0=h_tiles[a][:, j, :].rearrange("r (g p t) -> r g t p", g=PASSES, t=PACK),
                     scalar1=neg_mean[a][:, j : j + 1],
                     scalar2=rstd[a][:, j : j + 1],
                     op0=ALU.add,
@@ -149,8 +149,8 @@ def tile_toyattnsublayer_pa_t_kernel(
         def normalise_fourth_tile(a):
             for j in range(GPSIMD_TILES, TILES):
                 nc.scalar.activation(
-                    out=xhat[a][:, j, :],
-                    in_=h_tiles[a][:, j, :],
+                    out=xhat[a][:, j, :].rearrange("r (g t p) -> r g t p", g=PASSES, t=PACK),
+                    in_=h_tiles[a][:, j, :].rearrange("r (g p t) -> r g t p", g=PASSES, t=PACK),
                     func=ACT.Identity,
                     scale=rstd[a][:, j : j + 1],
                     bias=neg_mean_rstd[a][:, j : j + 1],
@@ -163,7 +163,7 @@ def tile_toyattnsublayer_pa_t_kernel(
                 for j in range(TILES):
                     nc.tensor.transpose(
                         xt[:, j * P : (j + 1) * P],
-                        xhat[a][:, j, g * K_PASS + t : (g + 1) * K_PASS : PACK],
+                        xhat[a][:, j, (g * PACK + t) * P : (g * PACK + t + 1) * P],
                         ident[:],
                     )
                 nc.scalar.activation(

@@ -29,8 +29,11 @@ GROUPS = ROWS_PER_PARTITION // TILES
 BN_CHUNK = 512
 BN_CHUNKS = D // BN_CHUNK
 HALF_TILES = TILES // 2
-GPSIMD_TILES = 3
-QUANTISE_LAG = 4
+TRANSPOSE_LAG = 2
+QUANTISE_LAG = 3
+PROJECT_LAG = 4
+SCALAR_REGROUP_TILES = 1
+SHARED_EXIT_GROUPS = 2
 
 
 def tile_toyattnsublayer_pa_t_kernel(
@@ -49,8 +52,8 @@ def tile_toyattnsublayer_pa_t_kernel(
         h_pool = ctx.enter_context(tc.tile_pool(name="h_pool", bufs=5))
         stat_pool = ctx.enter_context(tc.tile_pool(name="stat_pool", bufs=4))
         xhat_pool = ctx.enter_context(tc.tile_pool(name="xhat_pool", bufs=3))
-        plane_pool = ctx.enter_context(tc.tile_pool(name="plane_pool", bufs=(QUANTISE_LAG - 2) * PASSES))
-        grouped_pool = ctx.enter_context(tc.tile_pool(name="grouped_pool", bufs=PASSES))
+        plane_pool = ctx.enter_context(tc.tile_pool(name="plane_pool", bufs=2 * PASSES))
+        grouped_pool = ctx.enter_context(tc.tile_pool(name="grouped_pool", bufs=2 * PASSES))
         mx_pool = ctx.enter_context(tc.tile_pool(name="mx_pool", bufs=2))
         res_pool = ctx.enter_context(tc.tile_pool(name="res_pool", bufs=2))
         psum_t = ctx.enter_context(tc.psum_pool(name="psum_t", bufs=5))
@@ -65,6 +68,7 @@ def tile_toyattnsublayer_pa_t_kernel(
         accumulators = {}
         xhat = {}
         planes = {}
+        grouped = {}
         h_codes = {}
         h_scales = {}
 
@@ -119,42 +123,59 @@ def tile_toyattnsublayer_pa_t_kernel(
         def root(a):
             sd = stat_pool.tile([P, TILES], F32)
             nc.scalar.activation(out=sd[:], in_=mean_var[a][:, :, 1], func=ACT.Sqrt, bias=EPS, scale=1.0)
-            minus_mu = stat_pool.tile([P, TILES], F32)
-            nc.scalar.mul(out=minus_mu[:], in_=mean_var[a][:, :, 0], mul=-1.0)
             std[a] = sd
+
+        def negate_mean(a):
+            minus_mu = stat_pool.tile([P, TILES], F32)
+            nc.gpsimd.tensor_scalar(
+                out=minus_mu[:], in0=mean_var[a][:, :, 0], scalar1=-1.0, scalar2=0.0, op0=ALU.mult, op1=ALU.add
+            )
             neg_mean[a] = minus_mu
 
         def inverse(a):
             inv = stat_pool.tile([P, TILES], F32)
             nc.vector.reciprocal(out=inv[:], in_=std[a][:])
             minus_mu_rstd = stat_pool.tile([P, TILES], F32)
-            nc.vector.tensor_tensor(out=minus_mu_rstd[:], in0=neg_mean[a][:], in1=inv[:], op=ALU.mult)
+            nc.vector.scalar_tensor_tensor(
+                out=minus_mu_rstd[:], in0=mean_var[a][:, :, 0], scalar=-1.0, in1=inv[:], op0=ALU.mult, op1=ALU.mult
+            )
             rstd[a] = inv
             neg_mean_rstd[a] = minus_mu_rstd
 
-        def normalise_three_tiles(a):
-            engine = nc.vector if a == GROUPS - 1 else nc.gpsimd
-            xh = xhat_pool.tile([P, TILES, D], F32)
-            for j in range(GPSIMD_TILES):
-                engine.tensor_scalar(
-                    out=xh[:, j, :].rearrange("r (g t p) -> r g t p", g=PASSES, t=PACK),
-                    in0=h_tiles[a][:, j, :].rearrange("r (g p t) -> r g t p", g=PASSES, t=PACK),
-                    scalar1=neg_mean[a][:, j : j + 1],
-                    scalar2=rstd[a][:, j : j + 1],
-                    op0=ALU.add,
-                    op1=ALU.mult,
-                )
-            xhat[a] = xh
+        def normalise_plan(a):
+            if a == 0:
+                return [("gpsimd", 0, 0, 2), ("gpsimd", 1, 0, 2), ("scalar", 2, 0, 2), ("scalar", 3, 0, 2)]
+            if a == GROUPS - 1:
+                return [("vector", 0, 0, 2), ("vector", 1, 0, 2), ("vector", 2, 0, 2), ("scalar", 3, 0, 2)]
+            return [("gpsimd", 0, 0, 2), ("gpsimd", 1, 0, 2), ("gpsimd", 2, 0, 2), ("gpsimd", 3, 0, 1), ("scalar", 3, 1, 1)]
 
-        def normalise_fourth_tile(a):
-            for j in range(GPSIMD_TILES, TILES):
-                nc.scalar.activation(
-                    out=xhat[a][:, j, :].rearrange("r (g t p) -> r g t p", g=PASSES, t=PACK),
-                    in_=h_tiles[a][:, j, :].rearrange("r (g p t) -> r g t p", g=PASSES, t=PACK),
-                    func=ACT.Identity,
-                    scale=rstd[a][:, j : j + 1],
-                    bias=neg_mean_rstd[a][:, j : j + 1],
-                )
+        def normalise(a, on_scalar):
+            if a not in xhat:
+                xhat[a] = xhat_pool.tile([P, TILES, D], F32, name="xh")
+            for who, j, g0, n in normalise_plan(a):
+                if (who == "scalar") != on_scalar:
+                    continue
+                cols = slice(g0 * K_PASS, (g0 + n) * K_PASS)
+                dst = xhat[a][:, j, cols].rearrange("r (g t p) -> r g t p", g=n, t=PACK)
+                src = h_tiles[a][:, j, cols].rearrange("r (g p t) -> r g t p", g=n, t=PACK)
+                if on_scalar:
+                    nc.scalar.activation(
+                        out=dst,
+                        in_=src,
+                        func=ACT.Identity,
+                        scale=rstd[a][:, j : j + 1],
+                        bias=neg_mean_rstd[a][:, j : j + 1],
+                    )
+                else:
+                    engine = nc.vector if who == "vector" else nc.gpsimd
+                    engine.tensor_scalar(
+                        out=dst,
+                        in0=src,
+                        scalar1=neg_mean[a][:, j : j + 1],
+                        scalar2=rstd[a][:, j : j + 1],
+                        op0=ALU.add,
+                        op1=ALU.mult,
+                    )
 
         def transpose_and_scale(a, g):
             plane = plane_pool.tile([P, PACK, GROUP_ROWS], BF16)
@@ -166,31 +187,46 @@ def tile_toyattnsublayer_pa_t_kernel(
                         xhat[a][:, j, (g * PACK + t) * P : (g * PACK + t + 1) * P],
                         ident[:],
                     )
-                nc.scalar.activation(
-                    out=plane[:, t, :],
-                    in_=xt[:],
-                    func=ACT.Identity,
-                    scale=gain[:, g, t : t + 1],
-                    bias=shift[:, g, t : t + 1],
-                )
+                if a >= GROUPS - SHARED_EXIT_GROUPS and t % 2 == 1:
+                    nc.vector.tensor_scalar(
+                        out=plane[:, t, :],
+                        in0=xt[:],
+                        scalar1=gain[:, g, t : t + 1],
+                        scalar2=shift[:, g, t : t + 1],
+                        op0=ALU.mult,
+                        op1=ALU.add,
+                    )
+                else:
+                    nc.scalar.activation(
+                        out=plane[:, t, :],
+                        in_=xt[:],
+                        func=ACT.Identity,
+                        scale=gain[:, g, t : t + 1],
+                        bias=shift[:, g, t : t + 1],
+                    )
             planes[(a, g)] = plane
+
+        def regroup(a, on_scalar):
+            split = (TILES - SCALAR_REGROUP_TILES) * P
+            rows = slice(split, GROUP_ROWS) if on_scalar else slice(0, split)
+            for g in range(PASSES):
+                if (a, g) not in grouped:
+                    grouped[(a, g)] = grouped_pool.tile([P, GROUP_ROWS, PACK], BF16, align_bytes=64, name="side_by_side")
+                dst = grouped[(a, g)][:, rows, :].rearrange("p (c i) t -> p c t i", i=4)
+                src = planes[(a, g)][:, :, rows].rearrange("p t (c i) -> p c t i", i=4)
+                if on_scalar:
+                    nc.scalar.copy(out=dst, in_=src)
+                else:
+                    nc.vector.tensor_copy(out=dst, in_=src)
 
         def quantise(a):
             codes = mx_pool.tile([P, PASSES, GROUP_ROWS], U32, align_bytes=64)
             scales = mx_pool.tile([P, PASSES, GROUP_ROWS], U8, align_bytes=64)
-            grouped = []
-            for g in range(PASSES):
-                side_by_side = grouped_pool.tile([P, GROUP_ROWS, PACK], BF16, align_bytes=64)
-                nc.vector.tensor_copy(
-                    out=side_by_side[:].rearrange("p (c i) t -> p c t i", i=4),
-                    in_=planes[(a, g)][:].rearrange("p t (c i) -> p c t i", i=4),
-                )
-                grouped.append(side_by_side)
             for g in range(PASSES):
                 nc.vector.quantize_mx(
                     out=codes[:, g, :].bitcast(FP8X4),
                     scales=scales[:, g, :],
-                    in_=grouped[g][:].rearrange("p r t -> p (r t)"),
+                    in_=grouped[(a, g)][:].rearrange("p r t -> p (r t)"),
                 )
             h_codes[a] = codes
             h_scales[a] = scales
@@ -214,31 +250,41 @@ def tile_toyattnsublayer_pa_t_kernel(
         def store(a):
             for o in range(n_out):
                 res = res_pool.tile([P, TILES, E], F32, name="res%d" % o)
-                nc.scalar.copy(out=res[:].rearrange("p j e -> p (j e)"), in_=accumulators[(a, o)][:])
+                if a == GROUPS - 1 and o == 1:
+                    nc.vector.tensor_copy(out=res[:].rearrange("p j e -> p (j e)"), in_=accumulators[(a, o)][:])
+                else:
+                    nc.scalar.copy(out=res[:].rearrange("p j e -> p (j e)"), in_=accumulators[(a, o)][:])
                 nc.sync.dma_start(out=out_rows[o][:, a * TILES : (a + 1) * TILES, :], in_=res[:])
 
         def in_range(a):
             return 0 <= a < GROUPS
 
         with tc.manual_schedule():
-            for step in range(GROUPS + QUANTISE_LAG + 1):
+            for step in range(GROUPS + PROJECT_LAG + 1):
                 if in_range(step + 2) and step + 2 >= 2:
                     load(step + 2)
                 if in_range(step - 1):
                     root(step - 1)
+                    negate_mean(step - 1)
                 if in_range(step - QUANTISE_LAG):
+                    regroup(step - QUANTISE_LAG, False)
                     quantise(step - QUANTISE_LAG)
                 if in_range(step - 1):
                     inverse(step - 1)
-                    normalise_three_tiles(step - 1)
+                    normalise(step - 1, False)
                 if in_range(step):
                     statistics(step)
+                scalar_first = step - 1 in (0, 1, GROUPS - 1)
+                if in_range(step - 1) and scalar_first:
+                    normalise(step - 1, True)
                 for half in range(PASSES):
-                    if in_range(step - 3):
-                        transpose_and_scale(step - 3, half)
-                    if in_range(step - QUANTISE_LAG - 1):
-                        project(step - QUANTISE_LAG - 1, half)
-                if in_range(step - QUANTISE_LAG - 1):
-                    store(step - QUANTISE_LAG - 1)
-                if in_range(step - 1):
-                    normalise_fourth_tile(step - 1)
+                    if in_range(step - TRANSPOSE_LAG):
+                        transpose_and_scale(step - TRANSPOSE_LAG, half)
+                    if half == 0 and in_range(step - 1) and not scalar_first:
+                        normalise(step - 1, True)
+                    if in_range(step - PROJECT_LAG):
+                        project(step - PROJECT_LAG, half)
+                if in_range(step + 1 - QUANTISE_LAG):
+                    regroup(step + 1 - QUANTISE_LAG, True)
+                if in_range(step - PROJECT_LAG):
+                    store(step - PROJECT_LAG)

@@ -62,7 +62,6 @@ def tile_toyattnsublayer_pa_t_kernel(
         h_tiles = {}
         mean_var = {}
         std = {}
-        neg_mean = {}
         rstd = {}
         neg_mean_rstd = {}
         accumulators = {}
@@ -125,13 +124,6 @@ def tile_toyattnsublayer_pa_t_kernel(
             nc.scalar.activation(out=sd[:], in_=mean_var[a][:, :, 1], func=ACT.Sqrt, bias=EPS, scale=1.0)
             std[a] = sd
 
-        def negate_mean(a):
-            minus_mu = stat_pool.tile([P, TILES], F32)
-            nc.gpsimd.tensor_scalar(
-                out=minus_mu[:], in0=mean_var[a][:, :, 0], scalar1=-1.0, scalar2=0.0, op0=ALU.mult, op1=ALU.add
-            )
-            neg_mean[a] = minus_mu
-
         def inverse(a):
             inv = stat_pool.tile([P, TILES], F32)
             nc.vector.reciprocal(out=inv[:], in_=std[a][:])
@@ -156,8 +148,8 @@ def tile_toyattnsublayer_pa_t_kernel(
                 if (who == "scalar") != on_scalar:
                     continue
                 cols = slice(g0 * K_PASS, (g0 + n) * K_PASS)
-                dst = xhat[a][:, j, cols].rearrange("r (g t p) -> r g t p", g=n, t=PACK)
-                src = h_tiles[a][:, j, cols].rearrange("r (g p t) -> r g t p", g=n, t=PACK)
+                dst = xhat[a][:, j, cols]
+                src = h_tiles[a][:, j, cols]
                 if on_scalar:
                     nc.scalar.activation(
                         out=dst,
@@ -171,10 +163,10 @@ def tile_toyattnsublayer_pa_t_kernel(
                     engine.tensor_scalar(
                         out=dst,
                         in0=src,
-                        scalar1=neg_mean[a][:, j : j + 1],
-                        scalar2=rstd[a][:, j : j + 1],
-                        op0=ALU.add,
-                        op1=ALU.mult,
+                        scalar1=rstd[a][:, j : j + 1],
+                        scalar2=neg_mean_rstd[a][:, j : j + 1],
+                        op0=ALU.mult,
+                        op1=ALU.add,
                     )
 
         def transpose_and_scale(a, g):
@@ -184,7 +176,7 @@ def tile_toyattnsublayer_pa_t_kernel(
                 for j in range(TILES):
                     nc.tensor.transpose(
                         xt[:, j * P : (j + 1) * P],
-                        xhat[a][:, j, (g * PACK + t) * P : (g * PACK + t + 1) * P],
+                        xhat[a][:, j, g * K_PASS + t : (g + 1) * K_PASS : PACK],
                         ident[:],
                     )
                 if a >= GROUPS - SHARED_EXIT_GROUPS and t % 2 == 1:
@@ -265,7 +257,6 @@ def tile_toyattnsublayer_pa_t_kernel(
                     load(step + 2)
                 if in_range(step - 1):
                     root(step - 1)
-                    negate_mean(step - 1)
                 if in_range(step - QUANTISE_LAG):
                     regroup(step - QUANTISE_LAG, False)
                     quantise(step - QUANTISE_LAG)

@@ -29,6 +29,7 @@ GROUPS = ROWS_PER_PARTITION // TILES
 BN_CHUNK = 512
 BN_CHUNKS = D // BN_CHUNK
 HALF_TILES = TILES // 2
+N_OUT = 3
 TRANSPOSE_LAG = 2
 QUANTISE_LAG = 3
 PROJECT_LAG = 4
@@ -42,7 +43,6 @@ def tile_toyattnsublayer_pa_t_kernel(
     nc = tc.nc
     weights = [(w_q_words, w_q_scales), (w_k_words, w_k_scales), (w_v_words, w_v_scales)]
     outs = [out_0, out_1, out_2]
-    n_out = len(outs)
 
     h_rows = h.rearrange("(p j) d -> p j d", j=ROWS_PER_PARTITION)
     out_rows = [o.rearrange("(p j) e -> p j e", j=ROWS_PER_PARTITION) for o in outs]
@@ -57,7 +57,7 @@ def tile_toyattnsublayer_pa_t_kernel(
         mx_pool = ctx.enter_context(tc.tile_pool(name="mx_pool", bufs=2))
         res_pool = ctx.enter_context(tc.tile_pool(name="res_pool", bufs=2))
         psum_t = ctx.enter_context(tc.psum_pool(name="psum_t", bufs=5))
-        psum_o = ctx.enter_context(tc.psum_pool(name="psum_o", bufs=1))
+        psum_o = ctx.enter_context(tc.psum_pool(name="psum_o", bufs=3))
 
         h_tiles = {}
         mean_var = {}
@@ -65,6 +65,7 @@ def tile_toyattnsublayer_pa_t_kernel(
         rstd = {}
         neg_mean_rstd = {}
         accumulators = {}
+        results = {}
         xhat = {}
         planes = {}
         grouped = {}
@@ -91,18 +92,18 @@ def tile_toyattnsublayer_pa_t_kernel(
         nc.vector.tensor_copy(out=gain[:], in_=w_bf[:])
         nc.vector.tensor_copy(out=shift[:], in_=b_bf[:])
 
-        w_codes = const.tile([P, PASSES, n_out, E], U32, align_bytes=64)
-        w_planes = const.tile([P, PASSES, n_out, E], U8, align_bytes=64)
-        nc.vector.memset(w_planes[:].rearrange("p g o n -> p (g o n)").bitcast(I32), 0)
-        for o in range(n_out):
+        w_codes = const.tile([P, PASSES, N_OUT * E], U32, align_bytes=64)
+        w_planes = const.tile([P, PASSES, N_OUT * E], U8, align_bytes=64)
+        nc.vector.memset(w_planes[:].rearrange("p g n -> p (g n)").bitcast(I32), 0)
+        for o in range(N_OUT):
             words, scales = weights[o]
             nc.sync.dma_start(
-                out=w_codes[:, :, o, :].bitcast(I32),
+                out=w_codes[:, :, o * E : (o + 1) * E].bitcast(I32),
                 in_=words.rearrange("g p n t -> p g (n t)").bitcast(I32),
             )
             for quadrant in range(4):
                 nc.sync.dma_start(
-                    out=w_planes[32 * quadrant : 32 * quadrant + 4, :, o, :].bitcast(I32),
+                    out=w_planes[32 * quadrant : 32 * quadrant + 4, :, o * E : (o + 1) * E].bitcast(I32),
                     in_=scales[:, 4 * quadrant : 4 * quadrant + 4, :].rearrange("g q n -> q g n").bitcast(I32),
                 )
 
@@ -127,11 +128,13 @@ def tile_toyattnsublayer_pa_t_kernel(
         def inverse(a):
             inv = stat_pool.tile([P, TILES], F32)
             nc.vector.reciprocal(out=inv[:], in_=std[a][:])
+            rstd[a] = inv
+
+        def offset(a):
             minus_mu_rstd = stat_pool.tile([P, TILES], F32)
             nc.vector.scalar_tensor_tensor(
-                out=minus_mu_rstd[:], in0=mean_var[a][:, :, 0], scalar=-1.0, in1=inv[:], op0=ALU.mult, op1=ALU.mult
+                out=minus_mu_rstd[:], in0=mean_var[a][:, :, 0], scalar=-1.0, in1=rstd[a][:], op0=ALU.mult, op1=ALU.mult
             )
-            rstd[a] = inv
             neg_mean_rstd[a] = minus_mu_rstd
 
         def normalise_plan(a):
@@ -211,42 +214,44 @@ def tile_toyattnsublayer_pa_t_kernel(
                 else:
                     nc.vector.tensor_copy(out=dst, in_=src)
 
-        def quantise(a):
-            codes = mx_pool.tile([P, PASSES, GROUP_ROWS], U32, align_bytes=64)
-            scales = mx_pool.tile([P, PASSES, GROUP_ROWS], U8, align_bytes=64)
-            for g in range(PASSES):
-                nc.vector.quantize_mx(
-                    out=codes[:, g, :].bitcast(FP8X4),
-                    scales=scales[:, g, :],
-                    in_=grouped[(a, g)][:].rearrange("p r t -> p (r t)"),
-                )
-            h_codes[a] = codes
-            h_scales[a] = scales
+        def quantise(a, g):
+            if g == 0:
+                h_codes[a] = mx_pool.tile([P, PASSES, GROUP_ROWS], U32, align_bytes=64, name="codes")
+                h_scales[a] = mx_pool.tile([P, PASSES, GROUP_ROWS], U8, align_bytes=64, name="scales")
+            nc.vector.quantize_mx(
+                out=h_codes[a][:, g, :].bitcast(FP8X4),
+                scales=h_scales[a][:, g, :],
+                in_=grouped[(a, g)][:].rearrange("p r t -> p (r t)"),
+            )
 
-        def project(a, half):
-            for o in range(n_out):
-                if half == 0:
-                    accumulators[(a, o)] = psum_o.tile([P, TILES * E], F32, name="acc%d" % o)
-                for j in range(half * HALF_TILES, (half + 1) * HALF_TILES):
-                    for g in range(PASSES):
-                        nc.tensor.matmul_mx(
-                            out=accumulators[(a, o)][:, j * E : (j + 1) * E],
-                            lhsT=h_codes[a][:, g, j * P : (j + 1) * P].bitcast(FP8X4),
-                            lhsT_scale=h_scales[a][:, g, j * P : (j + 1) * P],
-                            rhs=w_codes[:, g, o, :].bitcast(FP8X4),
-                            rhs_scale=w_planes[:, g, o, :],
-                            start=(g == 0),
-                            stop=(g == PASSES - 1),
-                        )
+        def project(a, j):
+            acc = psum_o.tile([P, N_OUT * E], F32, name="acc")
+            for first, width in ((0, 2 * E), (2 * E, E)):
+                for g in range(PASSES):
+                    nc.tensor.matmul_mx(
+                        out=acc[:, first : first + width],
+                        lhsT=h_codes[a][:, g, j * P : (j + 1) * P].bitcast(FP8X4),
+                        lhsT_scale=h_scales[a][:, g, j * P : (j + 1) * P],
+                        rhs=w_codes[:, g, first : first + width].bitcast(FP8X4),
+                        rhs_scale=w_planes[:, g, first : first + width],
+                        start=(g == 0),
+                        stop=(g == PASSES - 1),
+                    )
+            accumulators[(a, j)] = acc
+
+        def collect(a, j):
+            if j == 0:
+                results[a] = res_pool.tile([P, N_OUT, TILES, E], F32, name="res")
+            dst = results[a][:, :, j, :]
+            src = accumulators[(a, j)][:].rearrange("p (o e) -> p o e", o=N_OUT)
+            if a == GROUPS - 1 and j % 2 == 1:
+                nc.vector.tensor_copy(out=dst, in_=src)
+            else:
+                nc.scalar.copy(out=dst, in_=src)
 
         def store(a):
-            for o in range(n_out):
-                res = res_pool.tile([P, TILES, E], F32, name="res%d" % o)
-                if a == GROUPS - 1 and o == 1:
-                    nc.vector.tensor_copy(out=res[:].rearrange("p j e -> p (j e)"), in_=accumulators[(a, o)][:])
-                else:
-                    nc.scalar.copy(out=res[:].rearrange("p j e -> p (j e)"), in_=accumulators[(a, o)][:])
-                nc.sync.dma_start(out=out_rows[o][:, a * TILES : (a + 1) * TILES, :], in_=res[:])
+            for o in range(N_OUT):
+                nc.sync.dma_start(out=out_rows[o][:, a * TILES : (a + 1) * TILES, :], in_=results[a][:, o, :, :])
 
         def in_range(a):
             return 0 <= a < GROUPS
@@ -259,9 +264,13 @@ def tile_toyattnsublayer_pa_t_kernel(
                     root(step - 1)
                 if in_range(step - QUANTISE_LAG):
                     regroup(step - QUANTISE_LAG, False)
-                    quantise(step - QUANTISE_LAG)
+                    quantise(step - QUANTISE_LAG, 0)
                 if in_range(step - 1):
                     inverse(step - 1)
+                if in_range(step - QUANTISE_LAG):
+                    quantise(step - QUANTISE_LAG, 1)
+                if in_range(step - 1):
+                    offset(step - 1)
                     normalise(step - 1, False)
                 if in_range(step):
                     statistics(step)
@@ -273,9 +282,12 @@ def tile_toyattnsublayer_pa_t_kernel(
                         transpose_and_scale(step - TRANSPOSE_LAG, half)
                     if half == 0 and in_range(step - 1) and not scalar_first:
                         normalise(step - 1, True)
+                    if half == 1 and in_range(step + 1 - QUANTISE_LAG):
+                        regroup(step + 1 - QUANTISE_LAG, True)
                     if in_range(step - PROJECT_LAG):
-                        project(step - PROJECT_LAG, half)
-                if in_range(step + 1 - QUANTISE_LAG):
-                    regroup(step + 1 - QUANTISE_LAG, True)
+                        for j in range(half * HALF_TILES, (half + 1) * HALF_TILES):
+                            project(step - PROJECT_LAG, j)
+                        for j in range(half * HALF_TILES, (half + 1) * HALF_TILES):
+                            collect(step - PROJECT_LAG, j)
                 if in_range(step - PROJECT_LAG):
                     store(step - PROJECT_LAG)

@@ -55,7 +55,7 @@ def tile_toyattnsublayer_pa_t_kernel(
         plane_pool = ctx.enter_context(tc.tile_pool(name="plane_pool", bufs=2 * PASSES))
         grouped_pool = ctx.enter_context(tc.tile_pool(name="grouped_pool", bufs=2 * PASSES))
         mx_pool = ctx.enter_context(tc.tile_pool(name="mx_pool", bufs=2))
-        res_pool = ctx.enter_context(tc.tile_pool(name="res_pool", bufs=2))
+        res_pool = ctx.enter_context(tc.tile_pool(name="res_pool", bufs=3))
         psum_t = ctx.enter_context(tc.psum_pool(name="psum_t", bufs=5))
         psum_o = ctx.enter_context(tc.psum_pool(name="psum_o", bufs=3))
 
@@ -75,7 +75,11 @@ def tile_toyattnsublayer_pa_t_kernel(
         def load(a):
             h_sb = h_pool.tile([P, TILES, D], BF16)
             for j in range(TILES):
-                nc.sync.dma_start(out=h_sb[:, j, :], in_=h_rows[:, a * TILES + j, :])
+                pieces = BN_CHUNKS if a == 0 and j == 0 else 1
+                width = D // pieces
+                for c in range(pieces):
+                    cols = slice(c * width, (c + 1) * width)
+                    nc.sync.dma_start(out=h_sb[:, j, cols], in_=h_rows[:, a * TILES + j, cols])
             h_tiles[a] = h_sb
 
         load(0)
@@ -201,9 +205,9 @@ def tile_toyattnsublayer_pa_t_kernel(
                     )
             planes[(a, g)] = plane
 
-        def regroup(a, on_scalar):
+        def regroup(a, on_scalar, first=0, last=GROUP_ROWS):
             split = (TILES - SCALAR_REGROUP_TILES) * P
-            rows = slice(split, GROUP_ROWS) if on_scalar else slice(0, split)
+            rows = slice(max(first, split), last) if on_scalar else slice(first, min(last, split))
             for g in range(PASSES):
                 if (a, g) not in grouped:
                     grouped[(a, g)] = grouped_pool.tile([P, GROUP_ROWS, PACK], BF16, align_bytes=64, name="side_by_side")
@@ -214,14 +218,14 @@ def tile_toyattnsublayer_pa_t_kernel(
                 else:
                     nc.vector.tensor_copy(out=dst, in_=src)
 
-        def quantise(a, g):
-            if g == 0:
+        def quantise(a, g, first=0, last=GROUP_ROWS):
+            if a not in h_codes:
                 h_codes[a] = mx_pool.tile([P, PASSES, GROUP_ROWS], U32, align_bytes=64, name="codes")
                 h_scales[a] = mx_pool.tile([P, PASSES, GROUP_ROWS], U8, align_bytes=64, name="scales")
             nc.vector.quantize_mx(
-                out=h_codes[a][:, g, :].bitcast(FP8X4),
-                scales=h_scales[a][:, g, :],
-                in_=grouped[(a, g)][:].rearrange("p r t -> p (r t)"),
+                out=h_codes[a][:, g, first:last].bitcast(FP8X4),
+                scales=h_scales[a][:, g, first:last],
+                in_=grouped[(a, g)][:, first:last, :].rearrange("p r t -> p (r t)"),
             )
 
         def project(a, j):
@@ -249,9 +253,11 @@ def tile_toyattnsublayer_pa_t_kernel(
             else:
                 nc.scalar.copy(out=dst, in_=src)
 
-        def store(a):
+        def store(a, first=0, last=TILES):
             for o in range(N_OUT):
-                nc.sync.dma_start(out=out_rows[o][:, a * TILES : (a + 1) * TILES, :], in_=results[a][:, o, :, :])
+                nc.sync.dma_start(
+                    out=out_rows[o][:, a * TILES + first : a * TILES + last, :], in_=results[a][:, o, first:last, :]
+                )
 
         def in_range(a):
             return 0 <= a < GROUPS
@@ -262,13 +268,18 @@ def tile_toyattnsublayer_pa_t_kernel(
                     load(step + 2)
                 if in_range(step - 1):
                     root(step - 1)
-                if in_range(step - QUANTISE_LAG):
+                if in_range(step - QUANTISE_LAG) and step - QUANTISE_LAG < GROUPS - 1:
                     regroup(step - QUANTISE_LAG, False)
                     quantise(step - QUANTISE_LAG, 0)
                 if in_range(step - 1):
                     inverse(step - 1)
-                if in_range(step - QUANTISE_LAG):
+                if in_range(step - QUANTISE_LAG) and step - QUANTISE_LAG < GROUPS - 1:
                     quantise(step - QUANTISE_LAG, 1)
+                if step - QUANTISE_LAG == GROUPS - 1:
+                    for first in (0, GROUP_ROWS // 2):
+                        regroup(GROUPS - 1, False, first, first + GROUP_ROWS // 2)
+                        for g in range(PASSES):
+                            quantise(GROUPS - 1, g, first, first + GROUP_ROWS // 2)
                 if in_range(step - 1):
                     offset(step - 1)
                     normalise(step - 1, False)
@@ -289,5 +300,7 @@ def tile_toyattnsublayer_pa_t_kernel(
                             project(step - PROJECT_LAG, j)
                         for j in range(half * HALF_TILES, (half + 1) * HALF_TILES):
                             collect(step - PROJECT_LAG, j)
-                if in_range(step - PROJECT_LAG):
+                        if step - PROJECT_LAG == GROUPS - 1:
+                            store(GROUPS - 1, half * HALF_TILES, (half + 1) * HALF_TILES)
+                if in_range(step - PROJECT_LAG) and step - PROJECT_LAG < GROUPS - 1:
                     store(step - PROJECT_LAG)

@@ -33,7 +33,9 @@ N_OUT = 3
 TRANSPOSE_LAG = 2
 QUANTISE_LAG = 3
 PROJECT_LAG = 4
-SCALAR_REGROUP_TILES = 1
+SCALAR_REGROUP_ROWS = 128
+EARLY_GROUPS = 3
+EARLY_SCALAR_REGROUP_ROWS = 192
 SHARED_EXIT_GROUPS = 2
 
 
@@ -145,7 +147,7 @@ def tile_toyattnsublayer_pa_t_kernel(
             if a == 0:
                 return [("gpsimd", 0, 0, 2), ("gpsimd", 1, 0, 2), ("scalar", 2, 0, 2), ("scalar", 3, 0, 2)]
             if a == GROUPS - 1:
-                return [("vector", 0, 0, 2), ("vector", 1, 0, 2), ("vector", 2, 0, 2), ("scalar", 3, 0, 2)]
+                return [("gpsimd", 0, 0, 2), ("gpsimd", 1, 0, 2), ("vector", 2, 0, 2), ("scalar", 3, 0, 2)]
             return [("gpsimd", 0, 0, 2), ("gpsimd", 1, 0, 2), ("gpsimd", 2, 0, 2), ("gpsimd", 3, 0, 1), ("scalar", 3, 1, 1)]
 
         def normalise(a, on_scalar):
@@ -186,7 +188,7 @@ def tile_toyattnsublayer_pa_t_kernel(
                         xhat[a][:, j, g * K_PASS + t : (g + 1) * K_PASS : PACK],
                         ident[:],
                     )
-                if a >= GROUPS - SHARED_EXIT_GROUPS and t % 2 == 1:
+                if a >= GROUPS - SHARED_EXIT_GROUPS and t % 2 == 0:
                     nc.vector.tensor_scalar(
                         out=plane[:, t, :],
                         in0=xt[:],
@@ -206,8 +208,11 @@ def tile_toyattnsublayer_pa_t_kernel(
             planes[(a, g)] = plane
 
         def regroup(a, on_scalar, first=0, last=GROUP_ROWS):
-            split = (TILES - SCALAR_REGROUP_TILES) * P
+            scalar_rows = EARLY_SCALAR_REGROUP_ROWS if a < EARLY_GROUPS else 0 if a == GROUPS - 1 else SCALAR_REGROUP_ROWS
+            split = GROUP_ROWS - scalar_rows
             rows = slice(max(first, split), last) if on_scalar else slice(first, min(last, split))
+            if rows.start >= rows.stop:
+                return
             for g in range(PASSES):
                 if (a, g) not in grouped:
                     grouped[(a, g)] = grouped_pool.tile([P, GROUP_ROWS, PACK], BF16, align_bytes=64, name="side_by_side")
@@ -248,10 +253,7 @@ def tile_toyattnsublayer_pa_t_kernel(
                 results[a] = res_pool.tile([P, N_OUT, TILES, E], F32, name="res")
             dst = results[a][:, :, j, :]
             src = accumulators[(a, j)][:].rearrange("p (o e) -> p o e", o=N_OUT)
-            if a == GROUPS - 1 and j % 2 == 1:
-                nc.vector.tensor_copy(out=dst, in_=src)
-            else:
-                nc.scalar.copy(out=dst, in_=src)
+            nc.scalar.copy(out=dst, in_=src)
 
         def store(a, first=0, last=TILES):
             for o in range(N_OUT):

@@ -95,8 +95,8 @@ def tile_toyattnsublayer_pa_t_kernel(
         nc.sync.dma_start(out=b_bf[:], in_=ln_b.rearrange("(g p t) -> p g t", g=PASSES, t=PACK))
         gain = const.tile([P, PASSES, PACK], F32)
         shift = const.tile([P, PASSES, PACK], F32)
-        nc.vector.tensor_copy(out=gain[:], in_=w_bf[:])
-        nc.vector.tensor_copy(out=shift[:], in_=b_bf[:])
+        nc.gpsimd.tensor_copy(out=gain[:], in_=w_bf[:])
+        nc.gpsimd.tensor_copy(out=shift[:], in_=b_bf[:])
 
         w_codes = const.tile([P, PASSES, N_OUT * E], U32, align_bytes=64)
         w_planes = const.tile([P, PASSES, N_OUT * E], U8, align_bytes=64)

@@ -32,11 +32,11 @@ HALF_TILES = TILES // 2
 N_OUT = 3
 TRANSPOSE_LAG = 2
 QUANTISE_LAG = 3
-PROJECT_LAG = 4
-SCALAR_REGROUP_ROWS = 128
+PROJECT_LAG = 3
+SCALAR_REGROUP_ROWS = 112
 EARLY_GROUPS = 3
 EARLY_SCALAR_REGROUP_ROWS = 192
-SHARED_EXIT_GROUPS = 2
+TAIL_GROUPS = 2
 
 
 def tile_toyattnsublayer_pa_t_kernel(
@@ -147,19 +147,24 @@ def tile_toyattnsublayer_pa_t_kernel(
             if a == 0:
                 return [("gpsimd", 0, 0, 2), ("gpsimd", 1, 0, 2), ("scalar", 2, 0, 2), ("scalar", 3, 0, 2)]
             if a == GROUPS - 1:
-                return [("gpsimd", 0, 0, 2), ("gpsimd", 1, 0, 2), ("vector", 2, 0, 2), ("scalar", 3, 0, 2)]
+                return [("vector", 0, 0, 2), ("vector", 1, 0, 2), ("vector", 2, 0, 2), ("scalar", 3, 0, 2)]
+            if a == GROUPS - 2:
+                return [("gpsimd", 0, 0, 2), ("gpsimd", 1, 0, 2), ("gpsimd", 2, 0, 2), ("vector", 3, 0, 1), ("scalar", 3, 1, 1)]
             return [("gpsimd", 0, 0, 2), ("gpsimd", 1, 0, 2), ("gpsimd", 2, 0, 2), ("gpsimd", 3, 0, 1), ("scalar", 3, 1, 1)]
 
-        def normalise(a, on_scalar):
+        def normalise(a, whose):
             if a not in xhat:
                 xhat[a] = xhat_pool.tile([P, TILES, D], F32, name="xh")
             for who, j, g0, n in normalise_plan(a):
-                if (who == "scalar") != on_scalar:
+                if who not in whose:
                     continue
                 cols = slice(g0 * K_PASS, (g0 + n) * K_PASS)
                 dst = xhat[a][:, j, cols]
                 src = h_tiles[a][:, j, cols]
-                if on_scalar:
+                if a >= GROUPS - TAIL_GROUPS:
+                    dst = dst.rearrange("p (g t m) -> p g t m", t=PACK, m=P)
+                    src = src.rearrange("p (g m t) -> p g t m", m=P, t=PACK)
+                if who == "scalar":
                     nc.scalar.activation(
                         out=dst,
                         in_=src,
@@ -178,17 +183,19 @@ def tile_toyattnsublayer_pa_t_kernel(
                         op1=ALU.add,
                     )
 
-        def transpose_and_scale(a, g):
-            plane = plane_pool.tile([P, PACK, GROUP_ROWS], BF16)
-            for t in range(PACK):
+        def transpose_and_scale(a, g, ts=(0, 1, 2, 3), engine=None):
+            if (a, g) not in planes:
+                planes[(a, g)] = plane_pool.tile([P, PACK, GROUP_ROWS], BF16, name="plane")
+            plane = planes[(a, g)]
+            for t in ts:
                 xt = psum_t.tile([P, GROUP_ROWS], F32)
+                if a >= GROUPS - TAIL_GROUPS:
+                    cols = slice(g * K_PASS + t * P, g * K_PASS + (t + 1) * P)
+                else:
+                    cols = slice(g * K_PASS + t, (g + 1) * K_PASS, PACK)
                 for j in range(TILES):
-                    nc.tensor.transpose(
-                        xt[:, j * P : (j + 1) * P],
-                        xhat[a][:, j, g * K_PASS + t : (g + 1) * K_PASS : PACK],
-                        ident[:],
-                    )
-                if a >= GROUPS - SHARED_EXIT_GROUPS and t % 2 == 0:
+                    nc.tensor.transpose(xt[:, j * P : (j + 1) * P], xhat[a][:, j, cols], ident[:])
+                if engine == "vector":
                     nc.vector.tensor_scalar(
                         out=plane[:, t, :],
                         in0=xt[:],
@@ -205,15 +212,14 @@ def tile_toyattnsublayer_pa_t_kernel(
                         scale=gain[:, g, t : t + 1],
                         bias=shift[:, g, t : t + 1],
                     )
-            planes[(a, g)] = plane
 
-        def regroup(a, on_scalar, first=0, last=GROUP_ROWS):
-            scalar_rows = EARLY_SCALAR_REGROUP_ROWS if a < EARLY_GROUPS else 0 if a == GROUPS - 1 else SCALAR_REGROUP_ROWS
+        def regroup(a, on_scalar, first=0, last=GROUP_ROWS, passes=(0, 1)):
+            scalar_rows = (192, 192)[a] if a < len((192, 192)) else 0 if a >= GROUPS - TAIL_GROUPS else SCALAR_REGROUP_ROWS
             split = GROUP_ROWS - scalar_rows
             rows = slice(max(first, split), last) if on_scalar else slice(first, min(last, split))
             if rows.start >= rows.stop:
                 return
-            for g in range(PASSES):
+            for g in passes:
                 if (a, g) not in grouped:
                     grouped[(a, g)] = grouped_pool.tile([P, GROUP_ROWS, PACK], BF16, align_bytes=64, name="side_by_side")
                 dst = grouped[(a, g)][:, rows, :].rearrange("p (c i) t -> p c t i", i=4)
@@ -248,12 +254,15 @@ def tile_toyattnsublayer_pa_t_kernel(
                     )
             accumulators[(a, j)] = acc
 
-        def collect(a, j):
-            if j == 0:
+        def collect(a, j, engine="scalar"):
+            if a not in results:
                 results[a] = res_pool.tile([P, N_OUT, TILES, E], F32, name="res")
             dst = results[a][:, :, j, :]
             src = accumulators[(a, j)][:].rearrange("p (o e) -> p o e", o=N_OUT)
-            nc.scalar.copy(out=dst, in_=src)
+            if engine == "vector":
+                nc.vector.tensor_copy(out=dst, in_=src)
+            else:
+                nc.scalar.copy(out=dst, in_=src)
 
         def store(a, first=0, last=TILES):
             for o in range(N_OUT):
@@ -265,36 +274,30 @@ def tile_toyattnsublayer_pa_t_kernel(
             return 0 <= a < GROUPS
 
         with tc.manual_schedule():
-            for step in range(GROUPS + PROJECT_LAG + 1):
+            for step in range(GROUPS):
                 if in_range(step + 2) and step + 2 >= 2:
                     load(step + 2)
-                if in_range(step - 1):
-                    root(step - 1)
-                if in_range(step - QUANTISE_LAG) and step - QUANTISE_LAG < GROUPS - 1:
+                if in_range(step - QUANTISE_LAG):
                     regroup(step - QUANTISE_LAG, False)
                     quantise(step - QUANTISE_LAG, 0)
                 if in_range(step - 1):
                     inverse(step - 1)
-                if in_range(step - QUANTISE_LAG) and step - QUANTISE_LAG < GROUPS - 1:
+                if in_range(step - QUANTISE_LAG):
                     quantise(step - QUANTISE_LAG, 1)
-                if step - QUANTISE_LAG == GROUPS - 1:
-                    for first in (0, GROUP_ROWS // 2):
-                        regroup(GROUPS - 1, False, first, first + GROUP_ROWS // 2)
-                        for g in range(PASSES):
-                            quantise(GROUPS - 1, g, first, first + GROUP_ROWS // 2)
                 if in_range(step - 1):
                     offset(step - 1)
-                    normalise(step - 1, False)
-                if in_range(step):
-                    statistics(step)
-                scalar_first = step - 1 in (0, 1, GROUPS - 1)
+                    normalise(step - 1, ("gpsimd",))
+                statistics(step)
+                scalar_first = step - 1 in (0, 1)
                 if in_range(step - 1) and scalar_first:
-                    normalise(step - 1, True)
+                    normalise(step - 1, ("scalar",))
                 for half in range(PASSES):
                     if in_range(step - TRANSPOSE_LAG):
                         transpose_and_scale(step - TRANSPOSE_LAG, half)
                     if half == 0 and in_range(step - 1) and not scalar_first:
-                        normalise(step - 1, True)
+                        normalise(step - 1, ("scalar",))
+                    if half == 1:
+                        root(step)
                     if half == 1 and in_range(step + 1 - QUANTISE_LAG):
                         regroup(step + 1 - QUANTISE_LAG, True)
                     if in_range(step - PROJECT_LAG):
@@ -302,7 +305,60 @@ def tile_toyattnsublayer_pa_t_kernel(
                             project(step - PROJECT_LAG, j)
                         for j in range(half * HALF_TILES, (half + 1) * HALF_TILES):
                             collect(step - PROJECT_LAG, j)
-                        if step - PROJECT_LAG == GROUPS - 1:
-                            store(GROUPS - 1, half * HALF_TILES, (half + 1) * HALF_TILES)
-                if in_range(step - PROJECT_LAG) and step - PROJECT_LAG < GROUPS - 1:
+                if in_range(step - PROJECT_LAG):
                     store(step - PROJECT_LAG)
+            normalise(GROUPS - 2, ("vector",))
+            regroup((GROUPS - 1) - 2, False, 0, 512, (0,))
+            inverse((GROUPS - 1))
+            regroup((GROUPS - 1) - 2, False, 0, 512, (1,))
+            offset((GROUPS - 1))
+            normalise(GROUPS - 1, ("vector",))
+            quantise((GROUPS - 1) - 2, 0, 0, 512)
+            transpose_and_scale((GROUPS - 1) - 1, 0, (0, 1,), "scalar")
+            quantise((GROUPS - 1) - 2, 1, 0, 512)
+            normalise(GROUPS - 1, ("scalar",))
+            transpose_and_scale((GROUPS - 1) - 1, 0, (2, 3,), "scalar")
+            transpose_and_scale((GROUPS - 1) - 1, 1, (0, 1, 2,), "scalar")
+            transpose_and_scale((GROUPS - 1) - 1, 1, (3,), "scalar")
+            transpose_and_scale(GROUPS - 1, 0, (0, 1,), "scalar")
+            project((GROUPS - 1) - 2, 0)
+            collect((GROUPS - 1) - 2, 0, "scalar")
+            project((GROUPS - 1) - 2, 1)
+            collect((GROUPS - 1) - 2, 1, "scalar")
+            transpose_and_scale(GROUPS - 1, 0, (2, 3,), "scalar")
+            project((GROUPS - 1) - 2, 2)
+            collect((GROUPS - 1) - 2, 2, "scalar")
+            project((GROUPS - 1) - 2, 3)
+            collect((GROUPS - 1) - 2, 3, "scalar")
+            store((GROUPS - 1) - 2, 0, 4)
+            regroup((GROUPS - 1) - 1, False, 0, 512, (0,))
+            regroup((GROUPS - 1) - 1, False, 0, 512, (1,))
+            quantise((GROUPS - 1) - 1, 0, 0, 512)
+            transpose_and_scale(GROUPS - 1, 1, (0, 1, 2,), "scalar")
+            quantise((GROUPS - 1) - 1, 1, 0, 512)
+            transpose_and_scale(GROUPS - 1, 1, (3,), "vector")
+            project((GROUPS - 1) - 1, 0)
+            collect((GROUPS - 1) - 1, 0, "scalar")
+            project((GROUPS - 1) - 1, 1)
+            collect((GROUPS - 1) - 1, 1, "scalar")
+            regroup(GROUPS - 1, False, 0, 512, (0,))
+            project((GROUPS - 1) - 1, 2)
+            collect((GROUPS - 1) - 1, 2, "scalar")
+            project((GROUPS - 1) - 1, 3)
+            collect((GROUPS - 1) - 1, 3, "scalar")
+            store((GROUPS - 1) - 1, 0, 4)
+            quantise(GROUPS - 1, 0, 0, 512)
+            regroup(GROUPS - 1, False, 0, 256, (1,))
+            regroup(GROUPS - 1, False, 256, 512, (1,))
+            quantise(GROUPS - 1, 1, 0, 256)
+            quantise(GROUPS - 1, 1, 256, 512)
+            project(GROUPS - 1, 0)
+            collect(GROUPS - 1, 0, "scalar")
+            project(GROUPS - 1, 1)
+            collect(GROUPS - 1, 1, "vector")
+            store(GROUPS - 1, 0, 2)
+            project(GROUPS - 1, 2)
+            collect(GROUPS - 1, 2, "scalar")
+            project(GROUPS - 1, 3)
+            collect(GROUPS - 1, 3, "vector")
+            store(GROUPS - 1, 2, 4)

@@ -33,10 +33,12 @@ N_OUT = 3
 TRANSPOSE_LAG = 2
 QUANTISE_LAG = 3
 PROJECT_LAG = 3
-SCALAR_REGROUP_ROWS = 112
+SCALAR_REGROUP_ROWS = 128
 EARLY_GROUPS = 3
 EARLY_SCALAR_REGROUP_ROWS = 192
 TAIL_GROUPS = 2
+SHARED_STATISTICS = (0,)
+GPSIMD_COLUMNS = 512
 
 
 def tile_toyattnsublayer_pa_t_kernel(
@@ -118,13 +120,27 @@ def tile_toyattnsublayer_pa_t_kernel(
         def statistics(a):
             h_sb = h_tiles[a]
             chunk_stats = stat_pool.tile([P, TILES, BN_CHUNKS, 6], F32)
-            mv = stat_pool.tile([P, TILES, 2], F32)
-            for j in range(TILES):
+            if a not in mean_var:
+                mean_var[a] = stat_pool.tile([P, TILES, 2], F32, name="mv")
+            mv = mean_var[a]
+            for j in range(TILES - 1 if a in SHARED_STATISTICS else TILES):
                 for c in range(BN_CHUNKS):
                     nc.vector.bn_stats(out=chunk_stats[:, j, c, :], in_=h_sb[:, j, c * BN_CHUNK : (c + 1) * BN_CHUNK])
-            for j in range(TILES):
+            for j in range(TILES - 1 if a in SHARED_STATISTICS else TILES):
                 nc.vector.bn_aggr(out=mv[:, j, :], in_=chunk_stats[:, j, :, :].rearrange("p c s -> p (c s)"))
-            mean_var[a] = mv
+
+        def scalar_statistics(a):
+            j = TILES - 1
+            if a not in mean_var:
+                mean_var[a] = stat_pool.tile([P, TILES, 2], F32, name="mv")
+            minus_mu = stat_pool.tile([P, 1], F32)
+            swept = const.tile([P, D], BF16, name="swept")
+            row = h_tiles[a][:, j, :]
+            nc.scalar.activation(out=swept[:], in_=row, func=ACT.Identity, scale=-1.0 / (32 * D), accum_out=minus_mu[:])
+            nc.scalar.activation(
+                out=swept[:], in_=row, func=ACT.Square, scale=1.0 / 32, bias=minus_mu[:], accum_out=mean_var[a][:, j, 1:2]
+            )
+            nc.scalar.activation(out=mean_var[a][:, j, 0:1], in_=minus_mu[:], func=ACT.Identity, scale=-32.0)
 
         def root(a):
             sd = stat_pool.tile([P, TILES], F32)
@@ -145,22 +161,21 @@ def tile_toyattnsublayer_pa_t_kernel(
 
         def normalise_plan(a):
             if a == 0:
-                return [("gpsimd", 0, 0, 2), ("gpsimd", 1, 0, 2), ("scalar", 2, 0, 2), ("scalar", 3, 0, 2)]
+                return [("gpsimd", 0, 0, D), ("gpsimd", 1, 0, D), ("scalar", 2, 0, D), ("scalar", 3, 0, D)]
             if a == GROUPS - 1:
-                return [("vector", 0, 0, 2), ("vector", 1, 0, 2), ("vector", 2, 0, 2), ("scalar", 3, 0, 2)]
+                return [("vector", 0, 0, D), ("vector", 1, 0, D), ("vector", 2, 0, D), ("scalar", 3, 0, D)]
             if a == GROUPS - 2:
-                return [("gpsimd", 0, 0, 2), ("gpsimd", 1, 0, 2), ("gpsimd", 2, 0, 2), ("vector", 3, 0, 1), ("scalar", 3, 1, 1)]
-            return [("gpsimd", 0, 0, 2), ("gpsimd", 1, 0, 2), ("gpsimd", 2, 0, 2), ("gpsimd", 3, 0, 1), ("scalar", 3, 1, 1)]
+                return [("gpsimd", 0, 0, D), ("gpsimd", 1, 0, D), ("gpsimd", 2, 0, D), ("vector", 3, 0, K_PASS), ("scalar", 3, K_PASS, D)]
+            return [("gpsimd", 0, 0, D), ("gpsimd", 1, 0, D), ("gpsimd", 2, 0, D), ("gpsimd", 3, 0, GPSIMD_COLUMNS), ("scalar", 3, GPSIMD_COLUMNS, D)]
 
         def normalise(a, whose):
             if a not in xhat:
                 xhat[a] = xhat_pool.tile([P, TILES, D], F32, name="xh")
-            for who, j, g0, n in normalise_plan(a):
-                if who not in whose:
+            for who, j, first, last in normalise_plan(a):
+                if who not in whose or first == last:
                     continue
-                cols = slice(g0 * K_PASS, (g0 + n) * K_PASS)
-                dst = xhat[a][:, j, cols]
-                src = h_tiles[a][:, j, cols]
+                dst = xhat[a][:, j, first:last]
+                src = h_tiles[a][:, j, first:last]
                 if a >= GROUPS - TAIL_GROUPS:
                     dst = dst.rearrange("p (g t m) -> p g t m", t=PACK, m=P)
                     src = src.rearrange("p (g m t) -> p g t m", m=P, t=PACK)
@@ -214,7 +229,7 @@ def tile_toyattnsublayer_pa_t_kernel(
                     )
 
         def regroup(a, on_scalar, first=0, last=GROUP_ROWS, passes=(0, 1)):
-            scalar_rows = (192, 192)[a] if a < len((192, 192)) else 0 if a >= GROUPS - TAIL_GROUPS else SCALAR_REGROUP_ROWS
+            scalar_rows = (192, 192, 160)[a] if a < len((192, 192, 160)) else 0 if a >= GROUPS - TAIL_GROUPS else SCALAR_REGROUP_ROWS
             split = GROUP_ROWS - scalar_rows
             rows = slice(max(first, split), last) if on_scalar else slice(first, min(last, split))
             if rows.start >= rows.stop:
@@ -287,10 +302,16 @@ def tile_toyattnsublayer_pa_t_kernel(
                 if in_range(step - 1):
                     offset(step - 1)
                     normalise(step - 1, ("gpsimd",))
+                if step == 0 and 0 in SHARED_STATISTICS:
+                    scalar_statistics(0)
+                if step == 0 and 1 in SHARED_STATISTICS:
+                    scalar_statistics(1)
                 statistics(step)
                 scalar_first = step - 1 in (0, 1)
                 if in_range(step - 1) and scalar_first:
                     normalise(step - 1, ("scalar",))
+                if step == 1 and 2 in SHARED_STATISTICS:
+                    scalar_statistics(2)
                 for half in range(PASSES):
                     if in_range(step - TRANSPOSE_LAG):
                         transpose_and_scale(step - TRANSPOSE_LAG, half)
@@ -347,18 +368,19 @@ def tile_toyattnsublayer_pa_t_kernel(
             project((GROUPS - 1) - 1, 3)
             collect((GROUPS - 1) - 1, 3, "scalar")
             store((GROUPS - 1) - 1, 0, 4)
-            quantise(GROUPS - 1, 0, 0, 512)
             regroup(GROUPS - 1, False, 0, 256, (1,))
-            regroup(GROUPS - 1, False, 256, 512, (1,))
+            quantise(GROUPS - 1, 0, 0, 512)
             quantise(GROUPS - 1, 1, 0, 256)
-            quantise(GROUPS - 1, 1, 256, 512)
             project(GROUPS - 1, 0)
             collect(GROUPS - 1, 0, "scalar")
             project(GROUPS - 1, 1)
-            collect(GROUPS - 1, 1, "vector")
+            collect(GROUPS - 1, 1, "scalar")
             store(GROUPS - 1, 0, 2)
+            regroup(GROUPS - 1, False, 256, 512, (1,))
+            quantise(GROUPS - 1, 1, 256, 512)
             project(GROUPS - 1, 2)
             collect(GROUPS - 1, 2, "scalar")
             project(GROUPS - 1, 3)
             collect(GROUPS - 1, 3, "vector")
-            store(GROUPS - 1, 2, 4)
+            store(GROUPS - 1, 2, 3)
+            store(GROUPS - 1, 3, 4)

@@ -33,10 +33,13 @@ N_OUT = 3
 TRANSPOSE_LAG = 2
 QUANTISE_LAG = 3
 PROJECT_LAG = 3
-SCALAR_REGROUP_ROWS = 128
+SCALAR_ROWS = 64
 EARLY_GROUPS = 3
 EARLY_SCALAR_REGROUP_ROWS = 192
 TAIL_GROUPS = 2
+TENSOR_ROW = GROUP_ROWS // 2
+EARLY_ROWS = (96, 96)
+TWO_PASS_GROUPS = 0
 SHARED_STATISTICS = (0,)
 GPSIMD_COLUMNS = 512
 
@@ -57,10 +60,11 @@ def tile_toyattnsublayer_pa_t_kernel(
         stat_pool = ctx.enter_context(tc.tile_pool(name="stat_pool", bufs=4))
         xhat_pool = ctx.enter_context(tc.tile_pool(name="xhat_pool", bufs=3))
         plane_pool = ctx.enter_context(tc.tile_pool(name="plane_pool", bufs=2 * PASSES))
-        grouped_pool = ctx.enter_context(tc.tile_pool(name="grouped_pool", bufs=2 * PASSES))
+        grouped_pool = ctx.enter_context(tc.tile_pool(name="grouped_pool", bufs=2))
         mx_pool = ctx.enter_context(tc.tile_pool(name="mx_pool", bufs=2))
         res_pool = ctx.enter_context(tc.tile_pool(name="res_pool", bufs=3))
-        psum_t = ctx.enter_context(tc.psum_pool(name="psum_t", bufs=5))
+        psum_t = ctx.enter_context(tc.psum_pool(name="psum_t", bufs=4))
+        psum_i = ctx.enter_context(tc.psum_pool(name="psum_i", bufs=1))
         psum_o = ctx.enter_context(tc.psum_pool(name="psum_o", bufs=3))
 
         h_tiles = {}
@@ -73,6 +77,8 @@ def tile_toyattnsublayer_pa_t_kernel(
         xhat = {}
         planes = {}
         grouped = {}
+        banks = {}
+        chunks = {}
         h_codes = {}
         h_scales = {}
 
@@ -87,9 +93,12 @@ def tile_toyattnsublayer_pa_t_kernel(
             h_tiles[a] = h_sb
 
         load(0)
+        load(1)
 
         ident = const.tile([P, P], F32)
         make_identity(nc, ident[:])
+        ident_bf = const.tile([P, P], BF16)
+        make_identity(nc, ident_bf[:])
 
         w_bf = const.tile([P, PASSES, PACK], BF16)
         b_bf = const.tile([P, PASSES, PACK], BF16)
@@ -103,36 +112,36 @@ def tile_toyattnsublayer_pa_t_kernel(
         w_codes = const.tile([P, PASSES, N_OUT * E], U32, align_bytes=64)
         w_planes = const.tile([P, PASSES, N_OUT * E], U8, align_bytes=64)
         nc.vector.memset(w_planes[:].rearrange("p g n -> p (g n)").bitcast(I32), 0)
-        for o in range(N_OUT):
-            words, scales = weights[o]
-            nc.sync.dma_start(
-                out=w_codes[:, :, o * E : (o + 1) * E].bitcast(I32),
-                in_=words.rearrange("g p n t -> p g (n t)").bitcast(I32),
-            )
-            for quadrant in range(4):
+
+        def load_weights():
+            for o in range(N_OUT):
+                words, scales = weights[o]
                 nc.sync.dma_start(
-                    out=w_planes[32 * quadrant : 32 * quadrant + 4, :, o * E : (o + 1) * E].bitcast(I32),
-                    in_=scales[:, 4 * quadrant : 4 * quadrant + 4, :].rearrange("g q n -> q g n").bitcast(I32),
+                    out=w_codes[:, :, o * E : (o + 1) * E].bitcast(I32),
+                    in_=words.rearrange("g p n t -> p g (n t)").bitcast(I32),
                 )
+                for quadrant in range(4):
+                    nc.sync.dma_start(
+                        out=w_planes[32 * quadrant : 32 * quadrant + 4, :, o * E : (o + 1) * E].bitcast(I32),
+                        in_=scales[:, 4 * quadrant : 4 * quadrant + 4, :].rearrange("g q n -> q g n").bitcast(I32),
+                    )
 
-        load(1)
-
-        def statistics(a):
+        def statistics(a, first, last):
             h_sb = h_tiles[a]
-            chunk_stats = stat_pool.tile([P, TILES, BN_CHUNKS, 6], F32)
             if a not in mean_var:
                 mean_var[a] = stat_pool.tile([P, TILES, 2], F32, name="mv")
-            mv = mean_var[a]
-            for j in range(TILES - 1 if a in SHARED_STATISTICS else TILES):
+                chunks[a] = stat_pool.tile([P, TILES, BN_CHUNKS, 6], F32, name="chunk_stats")
+            for j in range(first, last):
                 for c in range(BN_CHUNKS):
-                    nc.vector.bn_stats(out=chunk_stats[:, j, c, :], in_=h_sb[:, j, c * BN_CHUNK : (c + 1) * BN_CHUNK])
-            for j in range(TILES - 1 if a in SHARED_STATISTICS else TILES):
-                nc.vector.bn_aggr(out=mv[:, j, :], in_=chunk_stats[:, j, :, :].rearrange("p c s -> p (c s)"))
+                    nc.vector.bn_stats(out=chunks[a][:, j, c, :], in_=h_sb[:, j, c * BN_CHUNK : (c + 1) * BN_CHUNK])
+            for j in range(first, last):
+                nc.vector.bn_aggr(out=mean_var[a][:, j, :], in_=chunks[a][:, j, :, :].rearrange("p c s -> p (c s)"))
 
         def scalar_statistics(a):
             j = TILES - 1
             if a not in mean_var:
                 mean_var[a] = stat_pool.tile([P, TILES, 2], F32, name="mv")
+                chunks[a] = stat_pool.tile([P, TILES, BN_CHUNKS, 6], F32, name="chunk_stats")
             minus_mu = stat_pool.tile([P, 1], F32)
             swept = const.tile([P, D], BF16, name="swept")
             row = h_tiles[a][:, j, :]
@@ -166,7 +175,13 @@ def tile_toyattnsublayer_pa_t_kernel(
                 return [("vector", 0, 0, D), ("vector", 1, 0, D), ("vector", 2, 0, D), ("scalar", 3, 0, D)]
             if a == GROUPS - 2:
                 return [("gpsimd", 0, 0, D), ("gpsimd", 1, 0, D), ("gpsimd", 2, 0, D), ("vector", 3, 0, K_PASS), ("scalar", 3, K_PASS, D)]
-            return [("gpsimd", 0, 0, D), ("gpsimd", 1, 0, D), ("gpsimd", 2, 0, D), ("gpsimd", 3, 0, GPSIMD_COLUMNS), ("scalar", 3, GPSIMD_COLUMNS, D)]
+            return [
+                ("gpsimd", 0, 0, D),
+                ("gpsimd", 1, 0, D),
+                ("gpsimd", 2, 0, D),
+                ("gpsimd", 3, 0, GPSIMD_COLUMNS),
+                ("scalar", 3, GPSIMD_COLUMNS, D),
+            ]
 
         def normalise(a, whose):
             if a not in xhat:
@@ -204,10 +219,10 @@ def tile_toyattnsublayer_pa_t_kernel(
             plane = planes[(a, g)]
             for t in ts:
                 xt = psum_t.tile([P, GROUP_ROWS], F32)
-                if a >= GROUPS - TAIL_GROUPS:
-                    cols = slice(g * K_PASS + t * P, g * K_PASS + (t + 1) * P)
-                else:
+                if a < GROUPS - TAIL_GROUPS:
                     cols = slice(g * K_PASS + t, (g + 1) * K_PASS, PACK)
+                else:
+                    cols = slice(g * K_PASS + t * P, g * K_PASS + (t + 1) * P)
                 for j in range(TILES):
                     nc.tensor.transpose(xt[:, j * P : (j + 1) * P], xhat[a][:, j, cols], ident[:])
                 if engine == "vector":
@@ -228,21 +243,41 @@ def tile_toyattnsublayer_pa_t_kernel(
                         bias=shift[:, g, t : t + 1],
                     )
 
-        def regroup(a, on_scalar, first=0, last=GROUP_ROWS, passes=(0, 1)):
-            scalar_rows = (192, 192, 160)[a] if a < len((192, 192, 160)) else 0 if a >= GROUPS - TAIL_GROUPS else SCALAR_REGROUP_ROWS
-            split = GROUP_ROWS - scalar_rows
-            rows = slice(max(first, split), last) if on_scalar else slice(first, min(last, split))
-            if rows.start >= rows.stop:
+        def side_by_side(a):
+            if a not in grouped:
+                grouped[a] = grouped_pool.tile([P, PASSES, GROUP_ROWS, PACK], BF16, align_bytes=64, name="side")
+            return grouped[a]
+
+        def regroup(a, who, first, last, passes=(0, 1)):
+            if first >= last:
                 return
             for g in passes:
-                if (a, g) not in grouped:
-                    grouped[(a, g)] = grouped_pool.tile([P, GROUP_ROWS, PACK], BF16, align_bytes=64, name="side_by_side")
-                dst = grouped[(a, g)][:, rows, :].rearrange("p (c i) t -> p c t i", i=4)
-                src = planes[(a, g)][:, :, rows].rearrange("p t (c i) -> p c t i", i=4)
-                if on_scalar:
+                dst = side_by_side(a)[:, g, first:last, :].rearrange("p (c i) t -> p c t i", i=4)
+                src = planes[(a, g)][:, :, first:last].rearrange("p t (c i) -> p c t i", i=4)
+                if who == "scalar":
                     nc.scalar.copy(out=dst, in_=src)
                 else:
                     nc.vector.tensor_copy(out=dst, in_=src)
+
+        def tensor_regroup(a, g=0):
+            bank = psum_i.tile([P, GROUP_ROWS - TENSOR_ROW, PACK], BF16, name="bank")
+            for first in range(TENSOR_ROW, GROUP_ROWS, P):
+                nc.tensor.matmul(
+                    bank[:, first - TENSOR_ROW : first - TENSOR_ROW + P, :],
+                    lhsT=ident_bf[:],
+                    rhs=planes[(a, g)][:, :, first : first + P].rearrange("p t r -> p r t"),
+                    start=True,
+                    stop=True,
+                )
+            banks[(a, g)] = bank
+
+        def empty_regroup(a, g=0, engine="scalar"):
+            dst = side_by_side(a)[:, g, TENSOR_ROW:GROUP_ROWS, :].rearrange("p r t -> p (r t)")
+            src = banks[(a, g)][:].rearrange("p r t -> p (r t)")
+            if engine == "vector":
+                nc.vector.tensor_copy(out=dst, in_=src)
+            else:
+                nc.scalar.copy(out=dst, in_=src)
 
         def quantise(a, g, first=0, last=GROUP_ROWS):
             if a not in h_codes:
@@ -251,7 +286,7 @@ def tile_toyattnsublayer_pa_t_kernel(
             nc.vector.quantize_mx(
                 out=h_codes[a][:, g, first:last].bitcast(FP8X4),
                 scales=h_scales[a][:, g, first:last],
-                in_=grouped[(a, g)][:, first:last, :].rearrange("p r t -> p (r t)"),
+                in_=grouped[a][:, g, first:last, :].rearrange("p r t -> p (r t)"),
             )
 
         def project(a, j):
@@ -285,53 +320,109 @@ def tile_toyattnsublayer_pa_t_kernel(
                     out=out_rows[o][:, a * TILES + first : a * TILES + last, :], in_=results[a][:, o, first:last, :]
                 )
 
+        def tensor_passes(a):
+            return (0, 1) if a < TWO_PASS_GROUPS else (0,)
+
+        def vector_rows(a, g):
+            if g == 0:
+                return TENSOR_ROW - (EARLY_ROWS[a] if a < len(EARLY_ROWS) else SCALAR_ROWS)
+            return TENSOR_ROW if g in tensor_passes(a) else GROUP_ROWS
+
         def in_range(a):
             return 0 <= a < GROUPS
 
         with tc.manual_schedule():
+            first_root = const.tile([P, 1], F32)
+            nc.vector.memset(first_root[:], 1.0)
+            nc.scalar.activation(out=first_root[:], in_=first_root[:], func=ACT.Sqrt, bias=0.0, scale=1.0)
             for step in range(GROUPS):
-                if in_range(step + 2) and step + 2 >= 2:
+                turn, lay, mult = step - TRANSPOSE_LAG, step - QUANTISE_LAG, step - PROJECT_LAG
+                if turn == 0:
+                    turn = -1
+                if in_range(step + 2):
                     load(step + 2)
-                if in_range(step - QUANTISE_LAG):
-                    regroup(step - QUANTISE_LAG, False)
-                    quantise(step - QUANTISE_LAG, 0)
+                if step == 0:
+                    load_weights()
+                if in_range(lay):
+                    for g in range(PASSES):
+                        regroup(lay, "vector", 0, vector_rows(lay, g), (g,))
+                    quantise(lay, 0, 0, GROUP_ROWS)
+                if step == 1:
+                    statistics(1, 0, 1)
                 if in_range(step - 1):
                     inverse(step - 1)
-                if in_range(step - QUANTISE_LAG):
-                    quantise(step - QUANTISE_LAG, 1)
+                if in_range(lay):
+                    quantise(lay, 1, 0, GROUP_ROWS)
                 if in_range(step - 1):
                     offset(step - 1)
                     normalise(step - 1, ("gpsimd",))
-                if step == 0 and 0 in SHARED_STATISTICS:
+                if step == 0:
                     scalar_statistics(0)
-                if step == 0 and 1 in SHARED_STATISTICS:
-                    scalar_statistics(1)
-                statistics(step)
+                    statistics(0, 0, TILES - 1)
+                else:
+                    statistics(step, 1 if step == 1 else 0, TILES)
                 scalar_first = step - 1 in (0, 1)
                 if in_range(step - 1) and scalar_first:
                     normalise(step - 1, ("scalar",))
-                if step == 1 and 2 in SHARED_STATISTICS:
-                    scalar_statistics(2)
-                for half in range(PASSES):
-                    if in_range(step - TRANSPOSE_LAG):
-                        transpose_and_scale(step - TRANSPOSE_LAG, half)
-                    if half == 0 and in_range(step - 1) and not scalar_first:
+                if step == 1:
+                    turn = 0
+                    if in_range(turn):
+                        transpose_and_scale(turn, 0, (0, 1,))
+                    root(step)
+                    if in_range(turn):
+                        transpose_and_scale(turn, 0, (2, 3,))
+                    if in_range(turn):
+                        transpose_and_scale(turn, 1, (0, 1,))
+                    if in_range(turn):
+                        tensor_regroup(turn)
+                    if in_range(turn):
+                        empty_regroup(turn)
+                    if in_range(turn):
+                        transpose_and_scale(turn, 1, (2, 3,))
+                    if in_range(turn) and 1 in tensor_passes(turn):
+                        tensor_regroup(turn, 1)
+                    if in_range(turn) and 1 in tensor_passes(turn):
+                        empty_regroup(turn, 1)
+                    if in_range(turn):
+                        regroup(turn, "scalar", vector_rows(turn, 0), TENSOR_ROW, (0,))
+                else:
+                    if in_range(turn):
+                        transpose_and_scale(turn, 0, (0, 1, 2, 3,))
+                    if in_range(step - 1) and not scalar_first:
                         normalise(step - 1, ("scalar",))
-                    if half == 1:
-                        root(step)
-                    if half == 1 and in_range(step + 1 - QUANTISE_LAG):
-                        regroup(step + 1 - QUANTISE_LAG, True)
-                    if in_range(step - PROJECT_LAG):
-                        for j in range(half * HALF_TILES, (half + 1) * HALF_TILES):
-                            project(step - PROJECT_LAG, j)
-                        for j in range(half * HALF_TILES, (half + 1) * HALF_TILES):
-                            collect(step - PROJECT_LAG, j)
-                if in_range(step - PROJECT_LAG):
-                    store(step - PROJECT_LAG)
+                    if in_range(mult):
+                        project(mult, 0)
+                    if in_range(mult):
+                        project(mult, 1)
+                    if in_range(mult):
+                        collect(mult, 0, "scalar")
+                    if in_range(mult):
+                        collect(mult, 1, "scalar")
+                    if in_range(turn):
+                        transpose_and_scale(turn, 1, (0, 1,))
+                    if in_range(turn):
+                        tensor_regroup(turn)
+                    if in_range(turn):
+                        regroup(turn, "scalar", vector_rows(turn, 0), TENSOR_ROW, (0,))
+                    if in_range(turn):
+                        transpose_and_scale(turn, 1, (2, 3,))
+                    if in_range(turn):
+                        empty_regroup(turn)
+                    root(step)
+                    if in_range(mult):
+                        project(mult, 2)
+                    if in_range(mult):
+                        project(mult, 3)
+                    if in_range(mult):
+                        collect(mult, 2, "scalar")
+                    if in_range(mult):
+                        collect(mult, 3, "scalar")
+                if in_range(mult):
+                    store(mult)
             normalise(GROUPS - 2, ("vector",))
-            regroup((GROUPS - 1) - 2, False, 0, 512, (0,))
+            regroup(GROUPS - 3, "vector", 0, vector_rows(GROUPS - 3, 0), (0,))
             inverse((GROUPS - 1))
-            regroup((GROUPS - 1) - 2, False, 0, 512, (1,))
+            regroup(GROUPS - 3, "vector", 0, vector_rows(GROUPS - 3, 1), (1,))
             offset((GROUPS - 1))
             normalise(GROUPS - 1, ("vector",))
             quantise((GROUPS - 1) - 2, 0, 0, 512)
@@ -340,35 +431,39 @@ def tile_toyattnsublayer_pa_t_kernel(
             normalise(GROUPS - 1, ("scalar",))
             transpose_and_scale((GROUPS - 1) - 1, 0, (2, 3,), "scalar")
             transpose_and_scale((GROUPS - 1) - 1, 1, (0, 1, 2,), "scalar")
+            tensor_regroup(GROUPS - 2)
+            empty_regroup(GROUPS - 2, 0, "scalar")
             transpose_and_scale((GROUPS - 1) - 1, 1, (3,), "scalar")
-            transpose_and_scale(GROUPS - 1, 0, (0, 1,), "scalar")
             project((GROUPS - 1) - 2, 0)
-            collect((GROUPS - 1) - 2, 0, "scalar")
             project((GROUPS - 1) - 2, 1)
-            collect((GROUPS - 1) - 2, 1, "scalar")
-            transpose_and_scale(GROUPS - 1, 0, (2, 3,), "scalar")
+            regroup(GROUPS - 2, "vector", 0, TENSOR_ROW, (0,))
+            collect((GROUPS - 1) - 2, 0, "vector")
+            collect((GROUPS - 1) - 2, 1, "vector")
+            transpose_and_scale(GROUPS - 1, 0, (0, 1,), "scalar")
             project((GROUPS - 1) - 2, 2)
-            collect((GROUPS - 1) - 2, 2, "scalar")
             project((GROUPS - 1) - 2, 3)
-            collect((GROUPS - 1) - 2, 3, "scalar")
-            store((GROUPS - 1) - 2, 0, 4)
-            regroup((GROUPS - 1) - 1, False, 0, 512, (0,))
-            regroup((GROUPS - 1) - 1, False, 0, 512, (1,))
+            transpose_and_scale(GROUPS - 1, 0, (2, 3,), "scalar")
+            regroup(GROUPS - 2, "vector", 0, GROUP_ROWS, (1,))
             quantise((GROUPS - 1) - 1, 0, 0, 512)
             transpose_and_scale(GROUPS - 1, 1, (0, 1, 2,), "scalar")
             quantise((GROUPS - 1) - 1, 1, 0, 512)
+            collect((GROUPS - 1) - 2, 2, "vector")
+            collect((GROUPS - 1) - 2, 3, "vector")
+            store((GROUPS - 1) - 2, 0, 4)
+            tensor_regroup(GROUPS - 1)
+            empty_regroup(GROUPS - 1, 0, "scalar")
             transpose_and_scale(GROUPS - 1, 1, (3,), "vector")
             project((GROUPS - 1) - 1, 0)
             collect((GROUPS - 1) - 1, 0, "scalar")
             project((GROUPS - 1) - 1, 1)
             collect((GROUPS - 1) - 1, 1, "scalar")
-            regroup(GROUPS - 1, False, 0, 512, (0,))
+            regroup(GROUPS - 1, "vector", 0, TENSOR_ROW, (0,))
             project((GROUPS - 1) - 1, 2)
             collect((GROUPS - 1) - 1, 2, "scalar")
             project((GROUPS - 1) - 1, 3)
             collect((GROUPS - 1) - 1, 3, "scalar")
             store((GROUPS - 1) - 1, 0, 4)
-            regroup(GROUPS - 1, False, 0, 256, (1,))
+            regroup(GROUPS - 1, "vector", 0, 256, (1,))
             quantise(GROUPS - 1, 0, 0, 512)
             quantise(GROUPS - 1, 1, 0, 256)
             project(GROUPS - 1, 0)
@@ -376,7 +471,7 @@ def tile_toyattnsublayer_pa_t_kernel(
             project(GROUPS - 1, 1)
             collect(GROUPS - 1, 1, "scalar")
             store(GROUPS - 1, 0, 2)
-            regroup(GROUPS - 1, False, 256, 512, (1,))
+            regroup(GROUPS - 1, "vector", 256, GROUP_ROWS, (1,))
             quantise(GROUPS - 1, 1, 256, 512)
             project(GROUPS - 1, 2)
             collect(GROUPS - 1, 2, "scalar")

@@ -38,10 +38,11 @@ EARLY_GROUPS = 3
 EARLY_SCALAR_REGROUP_ROWS = 192
 TAIL_GROUPS = 2
 TENSOR_ROW = GROUP_ROWS // 2
-EARLY_ROWS = (96, 96)
+EARLY_ROWS = (128, 32)
 TWO_PASS_GROUPS = 0
+SCALAR_TILE = 1
 SHARED_STATISTICS = (0,)
-GPSIMD_COLUMNS = 512
+GPSIMD_COLUMNS = 448
 
 
 def tile_toyattnsublayer_pa_t_kernel(
@@ -93,12 +94,6 @@ def tile_toyattnsublayer_pa_t_kernel(
             h_tiles[a] = h_sb
 
         load(0)
-        load(1)
-
-        ident = const.tile([P, P], F32)
-        make_identity(nc, ident[:])
-        ident_bf = const.tile([P, P], BF16)
-        make_identity(nc, ident_bf[:])
 
         w_bf = const.tile([P, PASSES, PACK], BF16)
         b_bf = const.tile([P, PASSES, PACK], BF16)
@@ -108,6 +103,13 @@ def tile_toyattnsublayer_pa_t_kernel(
         shift = const.tile([P, PASSES, PACK], F32)
         nc.gpsimd.tensor_copy(out=gain[:], in_=w_bf[:])
         nc.gpsimd.tensor_copy(out=shift[:], in_=b_bf[:])
+
+        load(1)
+
+        ident = const.tile([P, P], F32)
+        make_identity(nc, ident[:])
+        ident_bf = const.tile([P, P], BF16)
+        make_identity(nc, ident_bf[:])
 
         w_codes = const.tile([P, PASSES, N_OUT * E], U32, align_bytes=64)
         w_planes = const.tile([P, PASSES, N_OUT * E], U8, align_bytes=64)
@@ -126,19 +128,19 @@ def tile_toyattnsublayer_pa_t_kernel(
                         in_=scales[:, 4 * quadrant : 4 * quadrant + 4, :].rearrange("g q n -> q g n").bitcast(I32),
                     )
 
-        def statistics(a, first, last):
+        def statistics(a, tiles):
             h_sb = h_tiles[a]
             if a not in mean_var:
                 mean_var[a] = stat_pool.tile([P, TILES, 2], F32, name="mv")
                 chunks[a] = stat_pool.tile([P, TILES, BN_CHUNKS, 6], F32, name="chunk_stats")
-            for j in range(first, last):
+            for j in tiles:
                 for c in range(BN_CHUNKS):
                     nc.vector.bn_stats(out=chunks[a][:, j, c, :], in_=h_sb[:, j, c * BN_CHUNK : (c + 1) * BN_CHUNK])
-            for j in range(first, last):
+            for j in tiles:
                 nc.vector.bn_aggr(out=mean_var[a][:, j, :], in_=chunks[a][:, j, :, :].rearrange("p c s -> p (c s)"))
 
         def scalar_statistics(a):
-            j = TILES - 1
+            j = SCALAR_TILE
             if a not in mean_var:
                 mean_var[a] = stat_pool.tile([P, TILES, 2], F32, name="mv")
                 chunks[a] = stat_pool.tile([P, TILES, BN_CHUNKS, 6], F32, name="chunk_stats")
@@ -347,8 +349,6 @@ def tile_toyattnsublayer_pa_t_kernel(
                     for g in range(PASSES):
                         regroup(lay, "vector", 0, vector_rows(lay, g), (g,))
                     quantise(lay, 0, 0, GROUP_ROWS)
-                if step == 1:
-                    statistics(1, 0, 1)
                 if in_range(step - 1):
                     inverse(step - 1)
                 if in_range(lay):
@@ -358,9 +358,9 @@ def tile_toyattnsublayer_pa_t_kernel(
                     normalise(step - 1, ("gpsimd",))
                 if step == 0:
                     scalar_statistics(0)
-                    statistics(0, 0, TILES - 1)
+                    statistics(0, [j for j in range(TILES) if j != SCALAR_TILE])
                 else:
-                    statistics(step, 1 if step == 1 else 0, TILES)
+                    statistics(step, range(TILES))
                 scalar_first = step - 1 in (0, 1)
                 if in_range(step - 1) and scalar_first:
                     normalise(step - 1, ("scalar",))
@@ -372,17 +372,11 @@ def tile_toyattnsublayer_pa_t_kernel(
                     if in_range(turn):
                         transpose_and_scale(turn, 0, (2, 3,))
                     if in_range(turn):
-                        transpose_and_scale(turn, 1, (0, 1,))
+                        transpose_and_scale(turn, 1, (0, 1, 2, 3,))
                     if in_range(turn):
                         tensor_regroup(turn)
                     if in_range(turn):
                         empty_regroup(turn)
-                    if in_range(turn):
-                        transpose_and_scale(turn, 1, (2, 3,))
-                    if in_range(turn) and 1 in tensor_passes(turn):
-                        tensor_regroup(turn, 1)
-                    if in_range(turn) and 1 in tensor_passes(turn):
-                        empty_regroup(turn, 1)
                     if in_range(turn):
                         regroup(turn, "scalar", vector_rows(turn, 0), TENSOR_ROW, (0,))
                 else:

@@ -33,16 +33,14 @@ N_OUT = 3
 TRANSPOSE_LAG = 2
 QUANTISE_LAG = 3
 PROJECT_LAG = 3
-SCALAR_ROWS = 64
+SCALAR_ROWS = 128
 EARLY_GROUPS = 3
 EARLY_SCALAR_REGROUP_ROWS = 192
 TAIL_GROUPS = 2
-TENSOR_ROW = GROUP_ROWS // 2
-EARLY_ROWS = (128, 32)
-TWO_PASS_GROUPS = 0
+EARLY_ROWS = (256, 160)
 SCALAR_TILE = 1
 SHARED_STATISTICS = (0,)
-GPSIMD_COLUMNS = 448
+GPSIMD_COLUMNS = 512
 
 
 def tile_toyattnsublayer_pa_t_kernel(
@@ -64,8 +62,7 @@ def tile_toyattnsublayer_pa_t_kernel(
         grouped_pool = ctx.enter_context(tc.tile_pool(name="grouped_pool", bufs=2))
         mx_pool = ctx.enter_context(tc.tile_pool(name="mx_pool", bufs=2))
         res_pool = ctx.enter_context(tc.tile_pool(name="res_pool", bufs=3))
-        psum_t = ctx.enter_context(tc.psum_pool(name="psum_t", bufs=4))
-        psum_i = ctx.enter_context(tc.psum_pool(name="psum_i", bufs=1))
+        psum_t = ctx.enter_context(tc.psum_pool(name="psum_t", bufs=5))
         psum_o = ctx.enter_context(tc.psum_pool(name="psum_o", bufs=3))
 
         h_tiles = {}
@@ -78,7 +75,6 @@ def tile_toyattnsublayer_pa_t_kernel(
         xhat = {}
         planes = {}
         grouped = {}
-        banks = {}
         chunks = {}
         h_codes = {}
         h_scales = {}
@@ -108,8 +104,6 @@ def tile_toyattnsublayer_pa_t_kernel(
 
         ident = const.tile([P, P], F32)
         make_identity(nc, ident[:])
-        ident_bf = const.tile([P, P], BF16)
-        make_identity(nc, ident_bf[:])
 
         w_codes = const.tile([P, PASSES, N_OUT * E], U32, align_bytes=64)
         w_planes = const.tile([P, PASSES, N_OUT * E], U8, align_bytes=64)
@@ -261,26 +255,6 @@ def tile_toyattnsublayer_pa_t_kernel(
                 else:
                     nc.vector.tensor_copy(out=dst, in_=src)
 
-        def tensor_regroup(a, g=0):
-            bank = psum_i.tile([P, GROUP_ROWS - TENSOR_ROW, PACK], BF16, name="bank")
-            for first in range(TENSOR_ROW, GROUP_ROWS, P):
-                nc.tensor.matmul(
-                    bank[:, first - TENSOR_ROW : first - TENSOR_ROW + P, :],
-                    lhsT=ident_bf[:],
-                    rhs=planes[(a, g)][:, :, first : first + P].rearrange("p t r -> p r t"),
-                    start=True,
-                    stop=True,
-                )
-            banks[(a, g)] = bank
-
-        def empty_regroup(a, g=0, engine="scalar"):
-            dst = side_by_side(a)[:, g, TENSOR_ROW:GROUP_ROWS, :].rearrange("p r t -> p (r t)")
-            src = banks[(a, g)][:].rearrange("p r t -> p (r t)")
-            if engine == "vector":
-                nc.vector.tensor_copy(out=dst, in_=src)
-            else:
-                nc.scalar.copy(out=dst, in_=src)
-
         def quantise(a, g, first=0, last=GROUP_ROWS):
             if a not in h_codes:
                 h_codes[a] = mx_pool.tile([P, PASSES, GROUP_ROWS], U32, align_bytes=64, name="codes")
@@ -322,13 +296,8 @@ def tile_toyattnsublayer_pa_t_kernel(
                     out=out_rows[o][:, a * TILES + first : a * TILES + last, :], in_=results[a][:, o, first:last, :]
                 )
 
-        def tensor_passes(a):
-            return (0, 1) if a < TWO_PASS_GROUPS else (0,)
-
         def vector_rows(a, g):
-            if g == 0:
-                return TENSOR_ROW - (EARLY_ROWS[a] if a < len(EARLY_ROWS) else SCALAR_ROWS)
-            return TENSOR_ROW if g in tensor_passes(a) else GROUP_ROWS
+            return GROUP_ROWS - (EARLY_ROWS[a] if a < len(EARLY_ROWS) else SCALAR_ROWS)
 
         def in_range(a):
             return 0 <= a < GROUPS
@@ -374,11 +343,7 @@ def tile_toyattnsublayer_pa_t_kernel(
                     if in_range(turn):
                         transpose_and_scale(turn, 1, (0, 1, 2, 3,))
                     if in_range(turn):
-                        tensor_regroup(turn)
-                    if in_range(turn):
-                        empty_regroup(turn)
-                    if in_range(turn):
-                        regroup(turn, "scalar", vector_rows(turn, 0), TENSOR_ROW, (0,))
+                        regroup(turn, "scalar", vector_rows(turn, 0), GROUP_ROWS)
                 else:
                     if in_range(turn):
                         transpose_and_scale(turn, 0, (0, 1, 2, 3,))
@@ -393,16 +358,10 @@ def tile_toyattnsublayer_pa_t_kernel(
                     if in_range(mult):
                         collect(mult, 1, "scalar")
                     if in_range(turn):
-                        transpose_and_scale(turn, 1, (0, 1,))
-                    if in_range(turn):
-                        tensor_regroup(turn)
-                    if in_range(turn):
-                        regroup(turn, "scalar", vector_rows(turn, 0), TENSOR_ROW, (0,))
-                    if in_range(turn):
-                        transpose_and_scale(turn, 1, (2, 3,))
-                    if in_range(turn):
-                        empty_regroup(turn)
+                        transpose_and_scale(turn, 1, (0, 1, 2, 3,))
                     root(step)
+                    if in_range(turn):
+                        regroup(turn, "scalar", vector_rows(turn, 0), GROUP_ROWS)
                     if in_range(mult):
                         project(mult, 2)
                     if in_range(mult):
@@ -425,12 +384,10 @@ def tile_toyattnsublayer_pa_t_kernel(
             normalise(GROUPS - 1, ("scalar",))
             transpose_and_scale((GROUPS - 1) - 1, 0, (2, 3,), "scalar")
             transpose_and_scale((GROUPS - 1) - 1, 1, (0, 1, 2,), "scalar")
-            tensor_regroup(GROUPS - 2)
-            empty_regroup(GROUPS - 2, 0, "scalar")
             transpose_and_scale((GROUPS - 1) - 1, 1, (3,), "scalar")
             project((GROUPS - 1) - 2, 0)
             project((GROUPS - 1) - 2, 1)
-            regroup(GROUPS - 2, "vector", 0, TENSOR_ROW, (0,))
+            regroup(GROUPS - 2, "vector", 0, GROUP_ROWS, (0,))
             collect((GROUPS - 1) - 2, 0, "vector")
             collect((GROUPS - 1) - 2, 1, "vector")
             transpose_and_scale(GROUPS - 1, 0, (0, 1,), "scalar")
@@ -444,14 +401,12 @@ def tile_toyattnsublayer_pa_t_kernel(
             collect((GROUPS - 1) - 2, 2, "vector")
             collect((GROUPS - 1) - 2, 3, "vector")
             store((GROUPS - 1) - 2, 0, 4)
-            tensor_regroup(GROUPS - 1)
-            empty_regroup(GROUPS - 1, 0, "scalar")
             transpose_and_scale(GROUPS - 1, 1, (3,), "vector")
             project((GROUPS - 1) - 1, 0)
             collect((GROUPS - 1) - 1, 0, "scalar")
             project((GROUPS - 1) - 1, 1)
             collect((GROUPS - 1) - 1, 1, "scalar")
-            regroup(GROUPS - 1, "vector", 0, TENSOR_ROW, (0,))
+            regroup(GROUPS - 1, "vector", 0, GROUP_ROWS, (0,))
             project((GROUPS - 1) - 1, 2)
             collect((GROUPS - 1) - 1, 2, "scalar")
             project((GROUPS - 1) - 1, 3)

from contextlib import ExitStack

import concourse.mybir as mybir
from concourse.masks import make_identity

F32 = mybir.dt.float32
BF16 = mybir.dt.bfloat16
I32 = mybir.dt.int32
U32 = mybir.dt.uint32
U8 = mybir.dt.uint8
FP8X4 = mybir.dt.float8_e4m3fn_x4
ALU = mybir.AluOpType
ACT = mybir.ActivationFunctionType

T = 8192
D = 1024
E = 128
EPS = 1e-5
FLOPS = 2 * T * D * 3 * E

P = 128
PACK = 4
K_PASS = P * PACK
PASSES = D // K_PASS
ROWS_PER_PARTITION = T // P
TILES = 4
GROUP_ROWS = TILES * P
GROUPS = ROWS_PER_PARTITION // TILES
BN_CHUNK = 512
BN_CHUNKS = D // BN_CHUNK
HALF_TILES = TILES // 2
N_OUT = 3
TRANSPOSE_LAG = 2
QUANTISE_LAG = 3
PROJECT_LAG = 3
SCALAR_ROWS = 128
EARLY_GROUPS = 3
EARLY_SCALAR_REGROUP_ROWS = 192
TAIL_GROUPS = 2
EARLY_ROWS = (256, 160)
SCALAR_TILE = 1
SHARED_STATISTICS = (0,)
GPSIMD_COLUMNS = 512


def tile_toyattnsublayer_pa_t_kernel(
    tc, h, ln_w, ln_b, w_q_words, w_q_scales, w_k_words, w_k_scales, w_v_words, w_v_scales, out_0, out_1, out_2
):
    nc = tc.nc
    weights = [(w_q_words, w_q_scales), (w_k_words, w_k_scales), (w_v_words, w_v_scales)]
    outs = [out_0, out_1, out_2]

    h_rows = h.rearrange("(p j) d -> p j d", j=ROWS_PER_PARTITION)
    out_rows = [o.rearrange("(p j) e -> p j e", j=ROWS_PER_PARTITION) for o in outs]

    with ExitStack() as ctx:
        const = ctx.enter_context(tc.tile_pool(name="const", bufs=1))
        h_pool = ctx.enter_context(tc.tile_pool(name="h_pool", bufs=5))
        stat_pool = ctx.enter_context(tc.tile_pool(name="stat_pool", bufs=4))
        xhat_pool = ctx.enter_context(tc.tile_pool(name="xhat_pool", bufs=3))
        plane_pool = ctx.enter_context(tc.tile_pool(name="plane_pool", bufs=2 * PASSES))
        grouped_pool = ctx.enter_context(tc.tile_pool(name="grouped_pool", bufs=2))
        mx_pool = ctx.enter_context(tc.tile_pool(name="mx_pool", bufs=2))
        res_pool = ctx.enter_context(tc.tile_pool(name="res_pool", bufs=3))
        psum_t = ctx.enter_context(tc.psum_pool(name="psum_t", bufs=5))
        psum_o = ctx.enter_context(tc.psum_pool(name="psum_o", bufs=3))

        h_tiles = {}
        mean_var = {}
        std = {}
        rstd = {}
        neg_mean_rstd = {}
        accumulators = {}
        results = {}
        xhat = {}
        planes = {}
        grouped = {}
        chunks = {}
        h_codes = {}
        h_scales = {}

        def load(a):
            h_sb = h_pool.tile([P, TILES, D], BF16)
            for j in range(TILES):
                pieces = BN_CHUNKS if a == 0 and j == 0 else 1
                width = D // pieces
                for c in range(pieces):
                    cols = slice(c * width, (c + 1) * width)
                    nc.sync.dma_start(out=h_sb[:, j, cols], in_=h_rows[:, a * TILES + j, cols])
            h_tiles[a] = h_sb

        load(0)

        w_bf = const.tile([P, PASSES, PACK], BF16)
        b_bf = const.tile([P, PASSES, PACK], BF16)
        nc.sync.dma_start(out=w_bf[:], in_=ln_w.rearrange("(g p t) -> p g t", g=PASSES, t=PACK))
        nc.sync.dma_start(out=b_bf[:], in_=ln_b.rearrange("(g p t) -> p g t", g=PASSES, t=PACK))
        gain = const.tile([P, PASSES, PACK], F32)
        shift = const.tile([P, PASSES, PACK], F32)
        nc.gpsimd.tensor_copy(out=gain[:], in_=w_bf[:])
        nc.gpsimd.tensor_copy(out=shift[:], in_=b_bf[:])

        load(1)

        ident = const.tile([P, P], F32)
        make_identity(nc, ident[:])

        w_codes = const.tile([P, PASSES, N_OUT * E], U32, align_bytes=64)
        w_planes = const.tile([P, PASSES, N_OUT * E], U8, align_bytes=64)
        nc.vector.memset(w_planes[:].rearrange("p g n -> p (g n)").bitcast(I32), 0)

        def load_weights():
            for o in range(N_OUT):
                words, scales = weights[o]
                nc.sync.dma_start(
                    out=w_codes[:, :, o * E : (o + 1) * E].bitcast(I32),
                    in_=words.rearrange("g p n t -> p g (n t)").bitcast(I32),
                )
                for quadrant in range(4):
                    nc.sync.dma_start(
                        out=w_planes[32 * quadrant : 32 * quadrant + 4, :, o * E : (o + 1) * E].bitcast(I32),
                        in_=scales[:, 4 * quadrant : 4 * quadrant + 4, :].rearrange("g q n -> q g n").bitcast(I32),
                    )

        def statistics(a, tiles):
            h_sb = h_tiles[a]
            if a not in mean_var:
                mean_var[a] = stat_pool.tile([P, TILES, 2], F32, name="mv")
                chunks[a] = stat_pool.tile([P, TILES, BN_CHUNKS, 6], F32, name="chunk_stats")
            for j in tiles:
                for c in range(BN_CHUNKS):
                    nc.vector.bn_stats(out=chunks[a][:, j, c, :], in_=h_sb[:, j, c * BN_CHUNK : (c + 1) * BN_CHUNK])
            for j in tiles:
                nc.vector.bn_aggr(out=mean_var[a][:, j, :], in_=chunks[a][:, j, :, :].rearrange("p c s -> p (c s)"))

        def scalar_statistics(a):
            j = SCALAR_TILE
            if a not in mean_var:
                mean_var[a] = stat_pool.tile([P, TILES, 2], F32, name="mv")
                chunks[a] = stat_pool.tile([P, TILES, BN_CHUNKS, 6], F32, name="chunk_stats")
            minus_mu = stat_pool.tile([P, 1], F32)
            swept = const.tile([P, D], BF16, name="swept")
            row = h_tiles[a][:, j, :]
            nc.scalar.activation(out=swept[:], in_=row, func=ACT.Identity, scale=-1.0 / (32 * D), accum_out=minus_mu[:])
            nc.scalar.activation(
                out=swept[:], in_=row, func=ACT.Square, scale=1.0 / 32, bias=minus_mu[:], accum_out=mean_var[a][:, j, 1:2]
            )
            nc.scalar.activation(out=mean_var[a][:, j, 0:1], in_=minus_mu[:], func=ACT.Identity, scale=-32.0)

        def root(a):
            sd = stat_pool.tile([P, TILES], F32)
            nc.scalar.activation(out=sd[:], in_=mean_var[a][:, :, 1], func=ACT.Sqrt, bias=EPS, scale=1.0)
            std[a] = sd

        def inverse(a):
            inv = stat_pool.tile([P, TILES], F32)
            nc.vector.reciprocal(out=inv[:], in_=std[a][:])
            rstd[a] = inv

        def offset(a):
            minus_mu_rstd = stat_pool.tile([P, TILES], F32)
            nc.vector.scalar_tensor_tensor(
                out=minus_mu_rstd[:], in0=mean_var[a][:, :, 0], scalar=-1.0, in1=rstd[a][:], op0=ALU.mult, op1=ALU.mult
            )
            neg_mean_rstd[a] = minus_mu_rstd

        def normalise_plan(a):
            if a == 0:
                return [("gpsimd", 0, 0, D), ("gpsimd", 1, 0, D), ("scalar", 2, 0, D), ("scalar", 3, 0, D)]
            if a == GROUPS - 1:
                return [("vector", 0, 0, D), ("vector", 1, 0, D), ("vector", 2, 0, D), ("scalar", 3, 0, D)]
            if a == GROUPS - 2:
                return [("gpsimd", 0, 0, D), ("gpsimd", 1, 0, D), ("gpsimd", 2, 0, D), ("vector", 3, 0, K_PASS), ("scalar", 3, K_PASS, D)]
            return [
                ("gpsimd", 0, 0, D),
                ("gpsimd", 1, 0, D),
                ("gpsimd", 2, 0, D),
                ("gpsimd", 3, 0, GPSIMD_COLUMNS),
                ("scalar", 3, GPSIMD_COLUMNS, D),
            ]

        def normalise(a, whose):
            if a not in xhat:
                xhat[a] = xhat_pool.tile([P, TILES, D], F32, name="xh")
            for who, j, first, last in normalise_plan(a):
                if who not in whose or first == last:
                    continue
                dst = xhat[a][:, j, first:last]
                src = h_tiles[a][:, j, first:last]
                if a >= GROUPS - TAIL_GROUPS:
                    dst = dst.rearrange("p (g t m) -> p g t m", t=PACK, m=P)
                    src = src.rearrange("p (g m t) -> p g t m", m=P, t=PACK)
                if who == "scalar":
                    nc.scalar.activation(
                        out=dst,
                        in_=src,
                        func=ACT.Identity,
                        scale=rstd[a][:, j : j + 1],
                        bias=neg_mean_rstd[a][:, j : j + 1],
                    )
                else:
                    engine = nc.vector if who == "vector" else nc.gpsimd
                    engine.tensor_scalar(
                        out=dst,
                        in0=src,
                        scalar1=rstd[a][:, j : j + 1],
                        scalar2=neg_mean_rstd[a][:, j : j + 1],
                        op0=ALU.mult,
                        op1=ALU.add,
                    )

        def transpose_and_scale(a, g, ts=(0, 1, 2, 3), engine=None):
            if (a, g) not in planes:
                planes[(a, g)] = plane_pool.tile([P, PACK, GROUP_ROWS], BF16, name="plane")
            plane = planes[(a, g)]
            for t in ts:
                xt = psum_t.tile([P, GROUP_ROWS], F32)
                if a < GROUPS - TAIL_GROUPS:
                    cols = slice(g * K_PASS + t, (g + 1) * K_PASS, PACK)
                else:
                    cols = slice(g * K_PASS + t * P, g * K_PASS + (t + 1) * P)
                for j in range(TILES):
                    nc.tensor.transpose(xt[:, j * P : (j + 1) * P], xhat[a][:, j, cols], ident[:])
                if engine == "vector":
                    nc.vector.tensor_scalar(
                        out=plane[:, t, :],
                        in0=xt[:],
                        scalar1=gain[:, g, t : t + 1],
                        scalar2=shift[:, g, t : t + 1],
                        op0=ALU.mult,
                        op1=ALU.add,
                    )
                else:
                    nc.scalar.activation(
                        out=plane[:, t, :],
                        in_=xt[:],
                        func=ACT.Identity,
                        scale=gain[:, g, t : t + 1],
                        bias=shift[:, g, t : t + 1],
                    )

        def side_by_side(a):
            if a not in grouped:
                grouped[a] = grouped_pool.tile([P, PASSES, GROUP_ROWS, PACK], BF16, align_bytes=64, name="side")
            return grouped[a]

        def regroup(a, who, first, last, passes=(0, 1)):
            if first >= last:
                return
            for g in passes:
                dst = side_by_side(a)[:, g, first:last, :].rearrange("p (c i) t -> p c t i", i=4)
                src = planes[(a, g)][:, :, first:last].rearrange("p t (c i) -> p c t i", i=4)
                if who == "scalar":
                    nc.scalar.copy(out=dst, in_=src)
                else:
                    nc.vector.tensor_copy(out=dst, in_=src)

        def quantise(a, g, first=0, last=GROUP_ROWS):
            if a not in h_codes:
                h_codes[a] = mx_pool.tile([P, PASSES, GROUP_ROWS], U32, align_bytes=64, name="codes")
                h_scales[a] = mx_pool.tile([P, PASSES, GROUP_ROWS], U8, align_bytes=64, name="scales")
            nc.vector.quantize_mx(
                out=h_codes[a][:, g, first:last].bitcast(FP8X4),
                scales=h_scales[a][:, g, first:last],
                in_=grouped[a][:, g, first:last, :].rearrange("p r t -> p (r t)"),
            )

        def project(a, j):
            acc = psum_o.tile([P, N_OUT * E], F32, name="acc")
            for first, width in ((0, 2 * E), (2 * E, E)):
                for g in range(PASSES):
                    nc.tensor.matmul_mx(
                        out=acc[:, first : first + width],
                        lhsT=h_codes[a][:, g, j * P : (j + 1) * P].bitcast(FP8X4),
                        lhsT_scale=h_scales[a][:, g, j * P : (j + 1) * P],
                        rhs=w_codes[:, g, first : first + width].bitcast(FP8X4),
                        rhs_scale=w_planes[:, g, first : first + width],
                        start=(g == 0),
                        stop=(g == PASSES - 1),
                    )
            accumulators[(a, j)] = acc

        def collect(a, j, engine="scalar"):
            if a not in results:
                results[a] = res_pool.tile([P, N_OUT, TILES, E], F32, name="res")
            dst = results[a][:, :, j, :]
            src = accumulators[(a, j)][:].rearrange("p (o e) -> p o e", o=N_OUT)
            if engine == "vector":
                nc.vector.tensor_copy(out=dst, in_=src)
            else:
                nc.scalar.copy(out=dst, in_=src)

        def store(a, first=0, last=TILES):
            for o in range(N_OUT):
                nc.sync.dma_start(
                    out=out_rows[o][:, a * TILES + first : a * TILES + last, :], in_=results[a][:, o, first:last, :]
                )

        def vector_rows(a, g):
            return GROUP_ROWS - (EARLY_ROWS[a] if a < len(EARLY_ROWS) else SCALAR_ROWS)

        def in_range(a):
            return 0 <= a < GROUPS

        with tc.manual_schedule():
            first_root = const.tile([P, 1], F32)
            nc.vector.memset(first_root[:], 1.0)
            nc.scalar.activation(out=first_root[:], in_=first_root[:], func=ACT.Sqrt, bias=0.0, scale=1.0)
            for step in range(GROUPS):
                turn, lay, mult = step - TRANSPOSE_LAG, step - QUANTISE_LAG, step - PROJECT_LAG
                if turn == 0:
                    turn = -1
                if in_range(step + 2):
                    load(step + 2)
                if step == 0:
                    load_weights()
                if in_range(lay):
                    for g in range(PASSES):
                        regroup(lay, "vector", 0, vector_rows(lay, g), (g,))
                    quantise(lay, 0, 0, GROUP_ROWS)
                if in_range(step - 1):
                    inverse(step - 1)
                if in_range(lay):
                    quantise(lay, 1, 0, GROUP_ROWS)
                if in_range(step - 1):
                    offset(step - 1)
                    normalise(step - 1, ("gpsimd",))
                if step == 0:
                    scalar_statistics(0)
                    statistics(0, [j for j in range(TILES) if j != SCALAR_TILE])
                else:
                    statistics(step, range(TILES))
                scalar_first = step - 1 in (0, 1)
                if in_range(step - 1) and scalar_first:
                    normalise(step - 1, ("scalar",))
                if step == 1:
                    turn = 0
                    if in_range(turn):
                        transpose_and_scale(turn, 0, (0, 1,))
                    root(step)
                    if in_range(turn):
                        transpose_and_scale(turn, 0, (2, 3,))
                    if in_range(turn):
                        transpose_and_scale(turn, 1, (0, 1, 2, 3,))
                    if in_range(turn):
                        regroup(turn, "scalar", vector_rows(turn, 0), GROUP_ROWS)
                else:
                    if in_range(turn):
                        transpose_and_scale(turn, 0, (0, 1, 2, 3,))
                    if in_range(step - 1) and not scalar_first:
                        normalise(step - 1, ("scalar",))
                    if in_range(mult):
                        project(mult, 0)
                    if in_range(mult):
                        project(mult, 1)
                    if in_range(mult):
                        collect(mult, 0, "scalar")
                    if in_range(mult):
                        collect(mult, 1, "scalar")
                    if in_range(turn):
                        transpose_and_scale(turn, 1, (0, 1, 2, 3,))
                    root(step)
                    if in_range(turn):
                        regroup(turn, "scalar", vector_rows(turn, 0), GROUP_ROWS)
                    if in_range(mult):
                        project(mult, 2)
                    if in_range(mult):
                        project(mult, 3)
                    if in_range(mult):
                        collect(mult, 2, "scalar")
                    if in_range(mult):
                        collect(mult, 3, "scalar")
                if in_range(mult):
                    store(mult)
            normalise(GROUPS - 2, ("vector",))
            regroup(GROUPS - 3, "vector", 0, vector_rows(GROUPS - 3, 0), (0,))
            inverse((GROUPS - 1))
            regroup(GROUPS - 3, "vector", 0, vector_rows(GROUPS - 3, 1), (1,))
            offset((GROUPS - 1))
            normalise(GROUPS - 1, ("vector",))
            quantise((GROUPS - 1) - 2, 0, 0, 512)
            transpose_and_scale((GROUPS - 1) - 1, 0, (0, 1,), "scalar")
            quantise((GROUPS - 1) - 2, 1, 0, 512)
            normalise(GROUPS - 1, ("scalar",))
            transpose_and_scale((GROUPS - 1) - 1, 0, (2, 3,), "scalar")
            transpose_and_scale((GROUPS - 1) - 1, 1, (0, 1, 2,), "scalar")
            transpose_and_scale((GROUPS - 1) - 1, 1, (3,), "scalar")
            project((GROUPS - 1) - 2, 0)
            project((GROUPS - 1) - 2, 1)
            regroup(GROUPS - 2, "vector", 0, GROUP_ROWS, (0,))
            collect((GROUPS - 1) - 2, 0, "vector")
            collect((GROUPS - 1) - 2, 1, "vector")
            transpose_and_scale(GROUPS - 1, 0, (0, 1,), "scalar")
            project((GROUPS - 1) - 2, 2)
            project((GROUPS - 1) - 2, 3)
            transpose_and_scale(GROUPS - 1, 0, (2, 3,), "scalar")
            regroup(GROUPS - 2, "vector", 0, GROUP_ROWS, (1,))
            quantise((GROUPS - 1) - 1, 0, 0, 512)
            transpose_and_scale(GROUPS - 1, 1, (0, 1, 2,), "scalar")
            quantise((GROUPS - 1) - 1, 1, 0, 512)
            collect((GROUPS - 1) - 2, 2, "vector")
            collect((GROUPS - 1) - 2, 3, "vector")
            store((GROUPS - 1) - 2, 0, 4)
            transpose_and_scale(GROUPS - 1, 1, (3,), "vector")
            project((GROUPS - 1) - 1, 0)
            collect((GROUPS - 1) - 1, 0, "scalar")
            project((GROUPS - 1) - 1, 1)
            collect((GROUPS - 1) - 1, 1, "scalar")
            regroup(GROUPS - 1, "vector", 0, GROUP_ROWS, (0,))
            project((GROUPS - 1) - 1, 2)
            collect((GROUPS - 1) - 1, 2, "scalar")
            project((GROUPS - 1) - 1, 3)
            collect((GROUPS - 1) - 1, 3, "scalar")
            store((GROUPS - 1) - 1, 0, 4)
            regroup(GROUPS - 1, "vector", 0, 256, (1,))
            quantise(GROUPS - 1, 0, 0, 512)
            quantise(GROUPS - 1, 1, 0, 256)
            project(GROUPS - 1, 0)
            collect(GROUPS - 1, 0, "scalar")
            project(GROUPS - 1, 1)
            collect(GROUPS - 1, 1, "scalar")
            store(GROUPS - 1, 0, 2)
            regroup(GROUPS - 1, "vector", 256, GROUP_ROWS, (1,))
            quantise(GROUPS - 1, 1, 256, 512)
            project(GROUPS - 1, 2)
            collect(GROUPS - 1, 2, "scalar")
            project(GROUPS - 1, 3)
            collect(GROUPS - 1, 3, "vector")
            store(GROUPS - 1, 2, 3)
            store(GROUPS - 1, 3, 4)
